import numpy as np
import ml_dtypes


def mxq(x, axis, fmt="e4m3"):
    dtype, down = {"e4m3": (ml_dtypes.float8_e4m3fn, 7), "e5m2": (ml_dtypes.float8_e5m2, 14)}[fmt]
    v = np.moveaxis(np.asarray(x, np.float32).astype(ml_dtypes.bfloat16).astype(np.float64), axis, -1)
    blocks = v.reshape(v.shape[:-1] + (-1, 32))
    amax = np.abs(blocks).max(-1, keepdims=True)
    byte = np.maximum(np.where(amax > 0, np.frexp(amax)[1] - 1 + 127, 0) - down, 1)
    scale = np.exp2(byte - 127.0)
    codes = (blocks / scale).astype(np.float32).astype(dtype).astype(np.float64)
    return np.moveaxis((codes * scale).reshape(v.shape), -1, axis)


WIDE = False


def mx_kscale(k):
    if not WIDE:
        return np.ones(k)
    levels = np.array([10, -10, 5, -5, 0])
    a = np.random.permutation(np.resize(levels, k // 512 * 4)).reshape(k // 512, 4)
    idx = np.arange(k)
    return np.exp2(a[idx // 512, idx % 128 // 32])


BF16 = ml_dtypes.bfloat16


def bf(x):
    return np.asarray(x, np.float32).astype(BF16)


def f64(x):
    return np.asarray(x).astype(np.float64)


B, S, D, H, QK = 1, 1024, 1024, 2048, 128
EPS = 1e-5
R = np.sqrt(0.1 * S / np.sqrt(QK))


def silu(a):
    return a / (1.0 + np.exp(-a))


def setup_inputs():
    s = mx_kscale(D)
    return {
        "x": bf(np.random.standard_normal((B, S, D)) + 0.5 * np.random.standard_normal((B, S, 1))),
        "ln_w": bf((1.0 + 0.1 * np.random.standard_normal(D)) * s),
        "ln_b": bf(0.1 * np.random.standard_normal(D) * s),
        "W_hidden": bf(np.random.standard_normal((2 * H, D)) / np.sqrt(D) / s),
        "b_hidden": bf(0.1 * np.random.standard_normal(2 * H)),
        "W_qk": bf(np.random.standard_normal((QK, D)) / np.sqrt(D) / s),
        "b_qk": bf(0.1 * np.random.standard_normal(QK)),
        "gamma": bf(np.random.standard_normal((2, QK)) * R / 0.6),
        "beta": bf(np.random.standard_normal((2, QK)) * R * 0.3),
    }


def reference(x, ln_w, ln_b, W_hidden, b_hidden, W_qk, b_qk, gamma, beta):
    x = f64(x)
    mu = x.mean(-1, keepdims=True)
    var = np.square(x - mu).mean(-1, keepdims=True)
    normed = (x - mu) / np.sqrt(var + EPS) * f64(ln_w) + f64(ln_b)
    nq = mxq(normed, 2, "e4m3")
    hg = silu((nq @ mxq(f64(W_hidden), 1, "e4m3").T) + f64(b_hidden))
    v, gate = hg[..., :H], hg[..., H:]
    Z = silu((nq @ mxq(f64(W_qk), 1, "e4m3").T) + f64(b_qk))
    gamma, beta = f64(gamma), f64(beta)
    q = Z * gamma[0] + beta[0]
    k = Z * gamma[1] + beta[1]
    return v, gate, q, k

@@ -1,0 +1,326 @@
+from contextlib import ExitStack
+
+import concourse.mybir as mybir
+from concourse.masks import make_identity
+
+F32 = mybir.dt.float32
+BF16 = mybir.dt.bfloat16
+U32 = mybir.dt.uint32
+U8 = mybir.dt.uint8
+FP8X4 = mybir.dt.float8_e4m3fn_x4
+ACT = mybir.ActivationFunctionType
+ALU = mybir.AluOpType
+
+P = 128
+EPS = 1e-5
+FLOPS = 2 * 1024 * 1024 * (4096 + 128)
+
+
+def tile_gau_pb_kernel(
+    tc, x, ln_w, ln_b, W_hidden, b_hidden, W_qk, b_qk, gamma, beta, out_0, out_1, out_2, out_3
+):
+    nc = tc.nc
+    xv = x.rearrange("o (p m) k -> p (o m) k", m=8)
+    wv = W_hidden.rearrange("(c s q i) k -> c q s (i k)", c=8, s=2, i=2)
+    ov = [
+        out_0.rearrange("o (p m) f -> p (o m) f", m=8),
+        out_1.rearrange("o (p m) f -> p (o m) f", m=8),
+    ]
+    oq = [
+        out_2.rearrange("o (p m) f -> p (o m) f", m=8),
+        out_3.rearrange("o (p m) f -> p (o m) f", m=8),
+    ]
+
+    with ExitStack() as ctx:
+        const = ctx.enter_context(tc.tile_pool(name="const", bufs=1))
+        xhp = ctx.enter_context(tc.tile_pool(name="xhp", bufs=6))
+        plp = ctx.enter_context(tc.tile_pool(name="plp", bufs=2))
+        big = ctx.enter_context(tc.tile_pool(name="big", bufs=8))
+        gwp = ctx.enter_context(tc.tile_pool(name="gwp", bufs=2))
+        tp = ctx.enter_context(tc.psum_pool(name="tp", bufs=4))
+        accp = ctx.enter_context(tc.psum_pool(name="accp", bufs=4))
+        ctx.enter_context(tc.manual_schedule())
+
+        ident = const.tile([P, P], F32, name="ident")
+        make_identity(nc, ident[:])
+        vecs = const.tile([P, 256], BF16, name="vecs")
+        nc.vector.memset(vecs[:], 0.0)
+        rows = const.tile([P, 512], BF16, name="rows")
+        nc.vector.memset(rows[:], 0.0)
+        mhalf = const.tile([P, 8], F32, name="mhalf")
+        nc.vector.memset(mhalf[:], -0.5)
+        identb = const.tile([P, P], BF16, name="identb")
+        nc.vector.tensor_copy(out=identb[:], in_=ident[:])
+        nc.scalar.dma_start(out=vecs[0:4, :], in_=ln_w.rearrange("(a c) -> a c", a=4))
+        nc.scalar.dma_start(out=vecs[4:8, :], in_=ln_b.rearrange("(a c) -> a c", a=4))
+        nc.scalar.dma_start(out=rows[0:8, :], in_=b_hidden.rearrange("(c n) -> c n", c=8))
+        nc.scalar.dma_start(out=rows[8:9, 0:256], in_=gamma.rearrange("(o a) f -> o (a f)", o=1))
+        nc.scalar.dma_start(out=rows[8:9, 256:512], in_=beta.rearrange("(o a) f -> o (a f)", o=1))
+        nc.scalar.dma_start(out=rows[9:10, 0:128], in_=b_qk.rearrange("(o f) -> o f", o=1))
+        warm = const.tile([P, 8], F32, name="warm")
+        nc.scalar.activation(out=warm[:], in_=mhalf[:], func=ACT.Silu)
+
+        xr = const.tile([P, 8, 1024], BF16, name="xr")
+        for i in range(4):
+            nc.sync.dma_start(out=xr[:, 2 * i : 2 * i + 2, :], in_=xv[:, 2 * i : 2 * i + 2, :])
+        wq = const.tile([P, 1024], BF16, name="wq")
+        nc.sync.dma_start(out=wq[:], in_=W_qk)
+        wraw = []
+        for c in range(8):
+            t = big.tile([P, 4096], BF16, tag="big", name="wraw%d" % c)
+            nc.sync.dma_start(out=t[:].rearrange("p (s w) -> p s w", s=2), in_=wv[c])
+            wraw.append(t)
+
+        pv = accp.tile([P, 512], F32, tag="acc", name="pv")
+        nc.tensor.transpose(pv[:, 0:128], vecs[:].bitcast(F32), ident[:])
+        wb = const.tile([P, 16], F32, name="wb")
+        bias_bc = const.tile([P, 4096], BF16, name="bias_bc")
+        qkc = const.tile([P, 1024], F32, name="qkc")
+        for i in range(5):
+            pb = tp.tile([P, 1024], BF16, tag="tp", name="pb%d" % i)
+            for s in range(2):
+                r = 2 * i + s
+                nc.tensor.matmul(
+                    out=pb[:, 512 * s : 512 * s + 512],
+                    lhsT=identb[:, r : r + 1].to_broadcast([P, P]),
+                    rhs=rows[:],
+                    start=True,
+                    stop=True,
+                )
+            dst = bias_bc[:, 1024 * i : 1024 * i + 1024] if i < 4 else qkc[:]
+            nc.scalar.copy(out=dst, in_=pb[:])
+
+        stats = const.tile([P, 8, 12], F32, name="stats")
+        mv = const.tile([P, 8, 2], F32, name="mv")
+        ve = const.tile([P, 8], F32, name="ve")
+        negmu = const.tile([P, 8], F32, name="negmu")
+        rstd = const.tile([P, 8], F32, name="rstd")
+        xh = [None] * 8
+        planes = [None] * 2
+        gn = [const.tile([P, 4096], BF16, name="gn%d" % h, align_bytes=64) for h in range(2)]
+        cn = [const.tile([P, 1024], U32, name="cn%d" % h, align_bytes=64) for h in range(2)]
+        sn = [const.tile([P, 1024], U8, name="sn%d" % h, align_bytes=64) for h in range(2)]
+
+        def row_stats(m):
+            for s in range(2):
+                nc.vector.bn_stats(out=stats[:, m, 6 * s : 6 * s + 6], in_=xr[:, m, 512 * s : 512 * s + 512])
+            nc.vector.bn_aggr(out=mv[:, m, :], in_=stats[:, m, :])
+
+        def row_scalars(a, b):
+            nc.vector.tensor_scalar(out=ve[:, a:b], in0=mv[:, a:b, 1], scalar1=EPS, scalar2=None, op0=ALU.add)
+            nc.vector.tensor_scalar(out=negmu[:, a:b], in0=mv[:, a:b, 0], scalar1=-1.0, scalar2=None, op0=ALU.mult)
+
+        def row_rstd(a, b):
+            nc.gpsimd.tensor_tensor(out=rstd[:, a:b], in0=ve[:, a:b], in1=mhalf[:, a:b], op=ALU.pow)
+
+        def normalise(m):
+            t = xhp.tile([P, 1024], F32, tag="xh", name="xh%d" % m)
+            xh[m] = t
+            nc.gpsimd.tensor_scalar(
+                out=t[:].rearrange("p (a e q) -> p a e q", a=4, e=2),
+                in0=xr[:, m, :].rearrange("p (a q e) -> p a e q", a=4, e=2),
+                scalar1=negmu[:, m : m + 1],
+                scalar2=rstd[:, m : m + 1],
+                op0=ALU.add,
+                op1=ALU.mult,
+            )
+
+        def x_bunch(h, g, engines):
+            if g == 0:
+                planes[h] = plp.tile([P, 8, 512], BF16, tag="pl", name="planes%d" % h)
+            banks = []
+            for t in range(4):
+                j = 4 * g + t
+                bank = tp.tile([P, 512], F32, tag="tp", name="xb%d_%d" % (h, j))
+                for mm in range(4):
+                    nc.tensor.transpose(
+                        bank[:, 128 * mm : 128 * mm + 128], xh[4 * h + mm][:, 128 * j : 128 * j + 128], ident[:]
+                    )
+                banks.append(bank)
+            for t in range(4):
+                j = 4 * g + t
+                if engines[t] == "S":
+                    nc.scalar.activation(
+                        out=planes[h][:, j, :], in_=banks[t][:], func=ACT.Identity,
+                        bias=wb[:, 8 + j : 9 + j], scale=wb[:, j : j + 1],
+                    )
+                else:
+                    nc.vector.tensor_scalar(
+                        out=planes[h][:, j, :], in0=banks[t][:], scalar1=wb[:, j : j + 1], scalar2=wb[:, 8 + j : 9 + j],
+                        op0=ALU.mult, op1=ALU.add,
+                    )
+
+        def regroup(h, g):
+            nc.vector.tensor_copy(
+                out=gn[h][:].rearrange("p (g c i t) -> p g c t i", g=2, i=4, t=4)[:, g],
+                in_=planes[h][:, 4 * g : 4 * g + 4, :].rearrange("p t (c i) -> p c t i", i=4),
+            )
+
+        def quant_n(h):
+            nc.vector.quantize_mx(out=cn[h][:].bitcast(FP8X4), scales=sn[h][:], in_=gn[h][:])
+
+        cw = [const.tile([P, 1024], U32, name="cw%d" % c, align_bytes=64) for c in range(8)]
+        sw = [const.tile([P, 1024], U8, name="sw%d" % c, align_bytes=64) for c in range(8)]
+        cq = const.tile([P, 256], U32, name="cq", align_bytes=64)
+        sq = const.tile([P, 256], U8, name="sq", align_bytes=64)
+        gws = [None] * 8
+
+        def w_bunch(c, engines):
+            w32 = wraw[c][:].bitcast(F32)
+            gw = gwp.tile([P, 4096], BF16, tag="gw", name="gw%d" % c, align_bytes=64)
+            gws[c] = gw
+            gw32 = gw[:].bitcast(F32).rearrange("p (b q i u) -> p b q i u", b=4, i=2, u=2)
+            banks = []
+            for b in range(4):
+                g, a = b // 2, b % 2
+                bank = tp.tile([P, 512], F32, tag="tp", name="wb%d_%d" % (c, b))
+                for i in range(2):
+                    for u in range(2):
+                        col = (2 * a + i) * 512 + 256 * g + 128 * u
+                        s = 2 * i + u
+                        nc.tensor.transpose(bank[:, 128 * s : 128 * s + 128], w32[:, col : col + 128], ident[:])
+                banks.append(bank)
+            for b in range(4):
+                src = banks[b][:].rearrange("p (i u q) -> p q i u", i=2, u=2)
+                if engines[b] == "S":
+                    nc.scalar.copy(out=gw32[:, b], in_=src)
+                else:
+                    nc.vector.tensor_copy(out=gw32[:, b], in_=src)
+
+        def quant_w(c):
+            nc.vector.quantize_mx(out=cw[c][:].bitcast(FP8X4), scales=sw[c][:], in_=gws[c][:])
+
+        def prep_qk():
+            w32 = wq[:].bitcast(F32)
+            gq = const.tile([P, 1024], BF16, name="gq", align_bytes=64)
+            bank = tp.tile([P, 512], F32, tag="tp", name="qb")
+            for s in range(4):
+                nc.tensor.transpose(bank[:, 128 * s : 128 * s + 128], w32[:, 128 * s : 128 * s + 128], ident[:])
+            nc.scalar.copy(
+                out=gq[:].bitcast(F32).rearrange("p (g f u) -> p g f u", g=2, u=2),
+                in_=bank[:].rearrange("p (g u f) -> p g f u", g=2, u=2),
+            )
+            nc.vector.quantize_mx(out=cq[:].bitcast(FP8X4), scales=sq[:], in_=gq[:])
+
+        def unit(c, h):
+            z = big.tile([P, 2048], F32, tag="big", name="z%d_%d" % (c, h))
+            cc = c % 4
+            for mm in range(4):
+                acc = accp.tile([P, 512], F32, tag="acc", name="acc%d_%d_%d" % (c, h, mm))
+                for g in range(2):
+                    lo = 512 * g + 128 * mm
+                    nc.tensor.matmul_mx(
+                        out=acc[:],
+                        lhsT=cn[h][:, lo : lo + 128].bitcast(FP8X4),
+                        lhsT_scale=sn[h][:, lo : lo + 128],
+                        rhs=cw[c][:, 512 * g : 512 * g + 512].bitcast(FP8X4),
+                        rhs_scale=sw[c][:, 512 * g : 512 * g + 512],
+                        start=(g == 0),
+                        stop=(g == 1),
+                    )
+                nc.vector.tensor_tensor(
+                    out=z[:, 512 * mm : 512 * mm + 512], in0=acc[:], in1=bias_bc[:, 512 * c : 512 * c + 512], op=ALU.add
+                )
+                if mm % 2 == 1:
+                    pair = z[:, 512 * (mm - 1) : 512 * (mm + 1)]
+                    nc.scalar.activation(out=pair, in_=pair, func=ACT.Silu)
+                    m0 = 4 * h + mm - 1
+                    nc.sync.dma_start(
+                        out=ov[c // 4][:, m0 : m0 + 2, 512 * cc : 512 * cc + 512],
+                        in_=pair.rearrange("p (m f) -> p m f", m=2),
+                    )
+
+        zq = const.tile([P, 1024], F32, name="zq")
+
+        def unit_qk(h):
+            acc = accp.tile([P, 512], F32, tag="acc", name="accq%d" % h)
+            for mm in range(4):
+                for g in range(2):
+                    lo = 512 * g + 128 * mm
+                    nc.tensor.matmul_mx(
+                        out=acc[:, 128 * mm : 128 * mm + 128],
+                        lhsT=cn[h][:, lo : lo + 128].bitcast(FP8X4),
+                        lhsT_scale=sn[h][:, lo : lo + 128],
+                        rhs=cq[:, 128 * g : 128 * g + 128].bitcast(FP8X4),
+                        rhs_scale=sq[:, 128 * g : 128 * g + 128],
+                        start=(g == 0),
+                        stop=(g == 1),
+                    )
+            zs = zq[:, 512 * h : 512 * h + 512]
+            nc.vector.tensor_tensor(
+                out=zs.rearrange("p (m f) -> p m f", m=4),
+                in0=acc[:].rearrange("p (m f) -> p m f", m=4),
+                in1=qkc[:, 512:640].unsqueeze(1).to_broadcast([P, 4, 128]),
+                op=ALU.add,
+            )
+            nc.scalar.activation(out=zs, in_=zs, func=ACT.Silu)
+
+        qk = [None]
+
+        def qk_scale():
+            qk[0] = plp.tile([P, 2048], F32, tag="pl", name="qk")
+            z3 = zq[:].rearrange("p (m f) -> p m f", m=8)
+            for i in range(2):
+                o3 = qk[0][:, 1024 * i : 1024 * i + 1024].rearrange("p (m f) -> p m f", m=8)
+                nc.gpsimd.tensor_tensor(
+                    out=o3, in0=z3, in1=qkc[:, 128 * i : 128 * i + 128].unsqueeze(1).to_broadcast([P, 8, 128]), op=ALU.mult
+                )
+                nc.gpsimd.tensor_tensor(
+                    out=o3, in0=o3, in1=qkc[:, 256 + 128 * i : 384 + 128 * i].unsqueeze(1).to_broadcast([P, 8, 128]),
+                    op=ALU.add,
+                )
+
+        def qk_store():
+            for i in range(2):
+                nc.sync.dma_start(out=oq[i], in_=qk[0][:, 1024 * i : 1024 * i + 1024].rearrange("p (m f) -> p m f", m=8))
+
+        for p in range(4):
+            row_stats(2 * p)
+            row_stats(2 * p + 1)
+            row_scalars(2 * p, 2 * p + 2)
+            if p == 0:
+                nc.vector.tensor_copy(out=wb[:], in_=pv[:, 0:8].bitcast(BF16))
+            if p < 2:
+                row_rstd(2 * p, 2 * p + 2)
+                normalise(2 * p)
+                normalise(2 * p + 1)
+        w_bunch(0, "SSSS")
+        quant_w(0)
+        x_bunch(0, 0, "SSSV")
+        regroup(0, 0)
+        x_bunch(0, 1, "SSSV")
+        for p in range(2, 4):
+            row_rstd(2 * p, 2 * p + 2)
+            normalise(2 * p)
+            normalise(2 * p + 1)
+        regroup(0, 1)
+        quant_n(0)
+        w_bunch(1, "SSSS")
+        quant_w(1)
+        x_bunch(1, 0, "SSSS")
+        unit(0, 0)
+        regroup(1, 0)
+        x_bunch(1, 1, "SSSV")
+        unit(1, 0)
+        regroup(1, 1)
+        quant_n(1)
+        w_bunch(2, "SVSV")
+        prep_qk()
+        quant_w(2)
+        w_bunch(3, "SSSV")
+        unit(0, 1)
+        quant_w(3)
+        unit(1, 1)
+        for c in range(2, 8):
+            if c + 2 < 8:
+                w_bunch(c + 2, "SSSV")
+            unit(c, 0)
+            if c + 2 < 8:
+                quant_w(c + 2)
+            if c == 2:
+                unit_qk(0)
+                unit_qk(1)
+                qk_scale()
+            unit(c, 1)
+            if c == 4:
+                qk_store()

@@ -51,18 +51,20 @@ def tile_gau_pb_kernel(
         nc.vector.memset(mhalf[:], -0.5)
         identb = const.tile([P, P], BF16, name="identb")
         nc.vector.tensor_copy(out=identb[:], in_=ident[:])
+        xr = const.tile([P, 8, 1024], BF16, name="xr")
+        for lo, hi in ((0, 1), (1, 2), (2, 4)):
+            nc.sync.dma_start(out=xr[:, lo:hi, :], in_=xv[:, lo:hi, :])
         nc.scalar.dma_start(out=vecs[0:4, :], in_=ln_w.rearrange("(a c) -> a c", a=4))
         nc.scalar.dma_start(out=vecs[4:8, :], in_=ln_b.rearrange("(a c) -> a c", a=4))
         nc.scalar.dma_start(out=rows[0:8, :], in_=b_hidden.rearrange("(c n) -> c n", c=8))
+        for lo, hi in ((4, 6), (6, 8)):
+            nc.sync.dma_start(out=xr[:, lo:hi, :], in_=xv[:, lo:hi, :])
+        warm = const.tile([P, 8], F32, name="warm")
+        nc.scalar.activation(out=warm[:], in_=mhalf[:], func=ACT.Silu)
         nc.scalar.dma_start(out=rows[8:9, 0:256], in_=gamma.rearrange("(o a) f -> o (a f)", o=1))
         nc.scalar.dma_start(out=rows[8:9, 256:512], in_=beta.rearrange("(o a) f -> o (a f)", o=1))
         nc.scalar.dma_start(out=rows[9:10, 0:128], in_=b_qk.rearrange("(o f) -> o f", o=1))
-        warm = const.tile([P, 8], F32, name="warm")
-        nc.scalar.activation(out=warm[:], in_=mhalf[:], func=ACT.Silu)
 
-        xr = const.tile([P, 8, 1024], BF16, name="xr")
-        for i in range(4):
-            nc.sync.dma_start(out=xr[:, 2 * i : 2 * i + 2, :], in_=xv[:, 2 * i : 2 * i + 2, :])
         wq = const.tile([P, 1024], BF16, name="wq")
         nc.sync.dma_start(out=wq[:], in_=W_qk)
         wraw = []
@@ -113,10 +115,10 @@ def tile_gau_pb_kernel(
         def row_rstd(a, b):
             nc.gpsimd.tensor_tensor(out=rstd[:, a:b], in0=ve[:, a:b], in1=mhalf[:, a:b], op=ALU.pow)
 
-        def normalise(m):
+        def normalise(m, engine):
             t = xhp.tile([P, 1024], F32, tag="xh", name="xh%d" % m)
             xh[m] = t
-            nc.gpsimd.tensor_scalar(
+            engine.tensor_scalar(
                 out=t[:].rearrange("p (a e q) -> p a e q", a=4, e=2),
                 in0=xr[:, m, :].rearrange("p (a q e) -> p a e q", a=4, e=2),
                 scalar1=negmu[:, m : m + 1],
@@ -190,9 +192,10 @@ def tile_gau_pb_kernel(
         def quant_w(c):
             nc.vector.quantize_mx(out=cw[c][:].bitcast(FP8X4), scales=sw[c][:], in_=gws[c][:])
 
-        def prep_qk():
+        gq = const.tile([P, 1024], BF16, name="gq", align_bytes=64)
+
+        def qk_bunch():
             w32 = wq[:].bitcast(F32)
-            gq = const.tile([P, 1024], BF16, name="gq", align_bytes=64)
             bank = tp.tile([P, 512], F32, tag="tp", name="qb")
             for s in range(4):
                 nc.tensor.transpose(bank[:, 128 * s : 128 * s + 128], w32[:, 128 * s : 128 * s + 128], ident[:])
@@ -200,6 +203,8 @@ def tile_gau_pb_kernel(
                 out=gq[:].bitcast(F32).rearrange("p (g f u) -> p g f u", g=2, u=2),
                 in_=bank[:].rearrange("p (g u f) -> p g f u", g=2, u=2),
             )
+
+        def quant_qk():
             nc.vector.quantize_mx(out=cq[:].bitcast(FP8X4), scales=sq[:], in_=gq[:])
 
         def unit(c, h):
@@ -221,13 +226,14 @@ def tile_gau_pb_kernel(
                 nc.vector.tensor_tensor(
                     out=z[:, 512 * mm : 512 * mm + 512], in0=acc[:], in1=bias_bc[:, 512 * c : 512 * c + 512], op=ALU.add
                 )
-                if mm % 2 == 1:
-                    pair = z[:, 512 * (mm - 1) : 512 * (mm + 1)]
-                    nc.scalar.activation(out=pair, in_=pair, func=ACT.Silu)
-                    m0 = 4 * h + mm - 1
+                n = 1 if (c == 7 and h == 1 and mm >= 2) else 2 * (mm % 2)
+                if n > 0:
+                    first = mm + 1 - n
+                    part = z[:, 512 * first : 512 * (mm + 1)]
+                    nc.scalar.activation(out=part, in_=part, func=ACT.Silu)
                     nc.sync.dma_start(
-                        out=ov[c // 4][:, m0 : m0 + 2, 512 * cc : 512 * cc + 512],
-                        in_=pair.rearrange("p (m f) -> p m f", m=2),
+                        out=ov[c // 4][:, 4 * h + first : 4 * h + mm + 1, 512 * cc : 512 * cc + 512],
+                        in_=part.rearrange("p (m f) -> p m f", m=n),
                     )
 
         zq = const.tile([P, 1024], F32, name="zq")
@@ -278,49 +284,49 @@ def tile_gau_pb_kernel(
             row_stats(2 * p)
             row_stats(2 * p + 1)
             row_scalars(2 * p, 2 * p + 2)
+            row_rstd(2 * p, 2 * p + 2)
             if p == 0:
                 nc.vector.tensor_copy(out=wb[:], in_=pv[:, 0:8].bitcast(BF16))
             if p < 2:
-                row_rstd(2 * p, 2 * p + 2)
-                normalise(2 * p)
-                normalise(2 * p + 1)
+                normalise(2 * p, nc.gpsimd)
+                normalise(2 * p + 1, nc.gpsimd)
+        qk_bunch()
         w_bunch(0, "SSSS")
+        x_bunch(0, 0, "SSSS")
         quant_w(0)
-        x_bunch(0, 0, "SSSV")
+        quant_qk()
+        normalise(4, nc.vector)
+        x_bunch(0, 1, "VSVS")
+        normalise(6, nc.vector)
+        w_bunch(1, "SVSV")
         regroup(0, 0)
-        x_bunch(0, 1, "SSSV")
-        for p in range(2, 4):
-            row_rstd(2 * p, 2 * p + 2)
-            normalise(2 * p)
-            normalise(2 * p + 1)
         regroup(0, 1)
-        quant_n(0)
-        w_bunch(1, "SSSS")
+        w_bunch(2, "SSSS")
+        normalise(5, nc.gpsimd)
         quant_w(1)
-        x_bunch(1, 0, "SSSS")
-        unit(0, 0)
+        normalise(7, nc.gpsimd)
+        quant_n(0)
+        x_bunch(1, 0, "SSSV")
+        x_bunch(1, 1, "SSSS")
+        quant_w(2)
+        w_bunch(3, "SSSS")
         regroup(1, 0)
-        x_bunch(1, 1, "SSSV")
-        unit(1, 0)
         regroup(1, 1)
         quant_n(1)
-        w_bunch(2, "SVSV")
-        prep_qk()
-        quant_w(2)
-        w_bunch(3, "SSSV")
-        unit(0, 1)
+        w_bunch(4, "SSSS")
         quant_w(3)
-        unit(1, 1)
-        for c in range(2, 8):
-            if c + 2 < 8:
-                w_bunch(c + 2, "SSSV")
+        for c in range(8):
             unit(c, 0)
-            if c + 2 < 8:
-                quant_w(c + 2)
-            if c == 2:
+            if 3 <= c <= 5:
+                w_bunch(c + 2, "SSSS")
+            if c == 0:
+                quant_w(4)
+            if 4 <= c <= 6:
+                quant_w(c + 1)
+            unit(c, 1)
+            if c == 0:
                 unit_qk(0)
                 unit_qk(1)
                 qk_scale()
-            unit(c, 1)
-            if c == 4:
+            if c == 3:
                 qk_store()

@@ -57,6 +57,12 @@ def tile_gau_pb_kernel(
         nc.scalar.dma_start(out=vecs[0:4, :], in_=ln_w.rearrange("(a c) -> a c", a=4))
         nc.scalar.dma_start(out=vecs[4:8, :], in_=ln_b.rearrange("(a c) -> a c", a=4))
         nc.scalar.dma_start(out=rows[0:8, :], in_=b_hidden.rearrange("(c n) -> c n", c=8))
+        wraw = [big.tile([P, 4096], BF16, tag="big", name="wraw%d" % c) for c in range(8)]
+
+        def load_w(c):
+            nc.sync.dma_start(out=wraw[c][:].rearrange("p (s w) -> p s w", s=2), in_=wv[c])
+
+        load_w(0)
         for lo, hi in ((4, 6), (6, 8)):
             nc.sync.dma_start(out=xr[:, lo:hi, :], in_=xv[:, lo:hi, :])
         warm = const.tile([P, 8], F32, name="warm")
@@ -65,13 +71,11 @@ def tile_gau_pb_kernel(
         nc.scalar.dma_start(out=rows[8:9, 256:512], in_=beta.rearrange("(o a) f -> o (a f)", o=1))
         nc.scalar.dma_start(out=rows[9:10, 0:128], in_=b_qk.rearrange("(o f) -> o f", o=1))
 
+        load_w(1)
         wq = const.tile([P, 1024], BF16, name="wq")
         nc.sync.dma_start(out=wq[:], in_=W_qk)
-        wraw = []
-        for c in range(8):
-            t = big.tile([P, 4096], BF16, tag="big", name="wraw%d" % c)
-            nc.sync.dma_start(out=t[:].rearrange("p (s w) -> p s w", s=2), in_=wv[c])
-            wraw.append(t)
+        for c in range(2, 8):
+            load_w(c)
 
         pv = accp.tile([P, 512], F32, tag="acc", name="pv")
         nc.tensor.transpose(pv[:, 0:128], vecs[:].bitcast(F32), ident[:])
@@ -290,43 +294,47 @@ def tile_gau_pb_kernel(
             if p < 2:
                 normalise(2 * p, nc.gpsimd)
                 normalise(2 * p + 1, nc.gpsimd)
-        qk_bunch()
+            if p == 2:
+                normalise(5, nc.gpsimd)
         w_bunch(0, "SSSS")
-        x_bunch(0, 0, "SSSS")
-        quant_w(0)
-        quant_qk()
+        w_bunch(1, "SSSS")
         normalise(4, nc.vector)
-        x_bunch(0, 1, "VSVS")
+        x_bunch(0, 0, "SVSV")
+        x_bunch(0, 1, "SVSS")
+        normalise(7, nc.gpsimd)
+        qk_bunch()
         normalise(6, nc.vector)
-        w_bunch(1, "SVSV")
         regroup(0, 0)
         regroup(0, 1)
-        w_bunch(2, "SSSS")
-        normalise(5, nc.gpsimd)
-        quant_w(1)
-        normalise(7, nc.gpsimd)
+        quant_w(0)
+        x_bunch(1, 0, "SSSS")
         quant_n(0)
-        x_bunch(1, 0, "SSSV")
-        x_bunch(1, 1, "SSSS")
-        quant_w(2)
-        w_bunch(3, "SSSS")
         regroup(1, 0)
+        x_bunch(1, 1, "SSSV")
+        quant_w(1)
         regroup(1, 1)
+        w_bunch(2, "SSSS")
+        quant_qk()
+        w_bunch(3, "SSSS")
+        quant_w(2)
         quant_n(1)
         w_bunch(4, "SSSS")
         quant_w(3)
         for c in range(8):
             unit(c, 0)
-            if 3 <= c <= 5:
-                w_bunch(c + 2, "SSSS")
             if c == 0:
                 quant_w(4)
-            if 4 <= c <= 6:
-                quant_w(c + 1)
+                w_bunch(5, "SSSV")
+            if c == 1:
+                quant_w(5)
             unit(c, 1)
-            if c == 0:
+            if c == 1:
                 unit_qk(0)
                 unit_qk(1)
                 qk_scale()
+            if c == 4 or c == 5:
+                quant_w(c + 2)
+            if c == 3 or c == 4:
+                w_bunch(c + 3, "SSSV")
             if c == 3:
                 qk_store()

@@ -157,10 +157,12 @@ def tile_gau_pb_kernel(
                     )
 
         def regroup(h, g):
-            nc.vector.tensor_copy(
-                out=gn[h][:].rearrange("p (g c i t) -> p g c t i", g=2, i=4, t=4)[:, g],
-                in_=planes[h][:, 4 * g : 4 * g + 4, :].rearrange("p t (c i) -> p c t i", i=4),
-            )
+            dst = gn[h][:].rearrange("p (g c i t) -> p g c t i", g=2, i=4, t=4)[:, g]
+            src = planes[h][:, 4 * g : 4 * g + 4, :].rearrange("p t (c i) -> p c t i", i=4)
+            if h == 0:
+                nc.vector.tensor_copy(out=dst, in_=src)
+            else:
+                nc.gpsimd.tensor_scalar(out=dst, in0=src, scalar1=1.0, scalar2=0.0, op0=ALU.mult, op1=ALU.add)
 
         def quant_n(h):
             nc.vector.quantize_mx(out=cn[h][:].bitcast(FP8X4), scales=sn[h][:], in_=gn[h][:])
@@ -294,47 +296,55 @@ def tile_gau_pb_kernel(
             if p < 2:
                 normalise(2 * p, nc.gpsimd)
                 normalise(2 * p + 1, nc.gpsimd)
-            if p == 2:
-                normalise(5, nc.gpsimd)
         w_bunch(0, "SSSS")
-        w_bunch(1, "SSSS")
-        normalise(4, nc.vector)
-        x_bunch(0, 0, "SVSV")
+        quant_w(0)
+        x_bunch(0, 0, "SSSV")
         x_bunch(0, 1, "SVSS")
+        normalise(4, nc.vector)
+        w_bunch(1, "VVSS")
+        normalise(6, nc.gpsimd)
+        normalise(5, nc.gpsimd)
+        regroup(0, 0)
+        w_bunch(2, "SSVV")
         normalise(7, nc.gpsimd)
         qk_bunch()
-        normalise(6, nc.vector)
-        regroup(0, 0)
-        regroup(0, 1)
-        quant_w(0)
-        x_bunch(1, 0, "SSSS")
-        quant_n(0)
-        regroup(1, 0)
-        x_bunch(1, 1, "SSSV")
         quant_w(1)
-        regroup(1, 1)
-        w_bunch(2, "SSSS")
-        quant_qk()
+        x_bunch(1, 0, "SSVS")
         w_bunch(3, "SSSS")
+        regroup(0, 1)
+        quant_n(0)
+        x_bunch(1, 1, "SSSS")
+        regroup(1, 1)
         quant_w(2)
-        quant_n(1)
-        w_bunch(4, "SSSS")
         quant_w(3)
-        for c in range(8):
-            unit(c, 0)
-            if c == 0:
-                quant_w(4)
-                w_bunch(5, "SSSV")
-            if c == 1:
-                quant_w(5)
-            unit(c, 1)
-            if c == 1:
-                unit_qk(0)
-                unit_qk(1)
-                qk_scale()
-            if c == 4 or c == 5:
-                quant_w(c + 2)
-            if c == 3 or c == 4:
-                w_bunch(c + 3, "SSSV")
-            if c == 3:
-                qk_store()
+        unit(0, 0)
+        unit(1, 0)
+        regroup(1, 0)
+        quant_qk()
+        w_bunch(4, "SSSV")
+        unit(2, 0)
+        quant_n(1)
+        quant_w(4)
+        w_bunch(5, "SSSS")
+        unit_qk(0)
+        unit_qk(1)
+        qk_scale()
+        unit(0, 1)
+        unit(1, 1)
+        unit(2, 1)
+        unit(3, 0)
+        unit(3, 1)
+        unit(4, 0)
+        quant_w(5)
+        qk_store()
+        w_bunch(6, "SVSS")
+        unit(4, 1)
+        unit(5, 0)
+        quant_w(6)
+        w_bunch(7, "SSSS")
+        unit(5, 1)
+        unit(6, 0)
+        quant_w(7)
+        unit(6, 1)
+        unit(7, 0)
+        unit(7, 1)

@@ -15,6 +15,17 @@ P = 128
 EPS = 1e-5
 FLOPS = 2 * 1024 * 1024 * (4096 + 128)
 
+ORDER = """
+ld.x.0.1 ld.bh ld.vec ld.x.1.2 ld.x.2.4 ld.w.0 ld.x.4.6 ld.x.6.8 warm ld.w.1 ld.qkv ld.wq ld.w.2 ld.w.3 ld.w.4 ld.w.5 ld.w.6 ld.w.7
+bias.0.S bias.1.S bias.2.S bias.3.S pv
+st.0 st.1 scv.0.2 wb nm.0.G nm.1.G st.2 st.3 scv.2.4 nm.2.G nm.3.G st.4 st.5 scv.4.6 st.6 st.7 scv.6.8
+w.0.SSSS qw.0 bias.4.S xb.0.0.SSSV xb.0.1.SVSS nm.4.V w.1.VVSS nm.6.G nm.5.G rg.0.0.V w.2.SSVV nm.7.G qkb.S qw.1 xb.1.0.SSVS w.3.SSSS rg.0.1.V qn.0
+xb.1.1.SSSS rg.1.1.G qw.2 qw.3 u.0.0 u.1.0 rg.1.0.G qq w.4.SSSV u.2.0 qn.1 qw.4 w.5.SSSS uq.0 uq.1 qks u.0.1 u.1.1 u.2.1 u.3.0 u.3.1 u.4.0 qw.5 qkst
+w.6.SVSS u.4.1 u.5.0 qw.6 w.7.SSSS u.5.1 u.6.0 qw.7 u.6.1 u.7.0 u.7.1.211
+"""
+
+QKDT = F32 if "ld.qkv" in ORDER else BF16
+
 
 def tile_gau_pb_kernel(
     tc, x, ln_w, ln_b, W_hidden, b_hidden, W_qk, b_qk, gamma, beta, out_0, out_1, out_2, out_3
@@ -41,66 +52,84 @@ def tile_gau_pb_kernel(
         accp = ctx.enter_context(tc.psum_pool(name="accp", bufs=4))
         ctx.enter_context(tc.manual_schedule())
 
-        ident = const.tile([P, P], F32, name="ident")
-        make_identity(nc, ident[:])
-        vecs = const.tile([P, 256], BF16, name="vecs")
-        nc.vector.memset(vecs[:], 0.0)
+        eng = {"S": nc.scalar, "V": nc.vector, "G": nc.gpsimd}
+
         rows = const.tile([P, 512], BF16, name="rows")
         nc.vector.memset(rows[:], 0.0)
+        vecs = const.tile([P, 256], BF16, name="vecs")
+        nc.vector.memset(vecs[:], 0.0)
+        rowq = const.tile([P, 512], BF16, name="rowq")
+        if "ld.qkv" in ORDER:
+            nc.vector.memset(rowq[:], 0.0)
         mhalf = const.tile([P, 8], F32, name="mhalf")
         nc.vector.memset(mhalf[:], -0.5)
+        ident = const.tile([P, P], F32, name="ident")
+        make_identity(nc, ident[:])
         identb = const.tile([P, P], BF16, name="identb")
         nc.vector.tensor_copy(out=identb[:], in_=ident[:])
         xr = const.tile([P, 8, 1024], BF16, name="xr")
-        for lo, hi in ((0, 1), (1, 2), (2, 4)):
-            nc.sync.dma_start(out=xr[:, lo:hi, :], in_=xv[:, lo:hi, :])
-        nc.scalar.dma_start(out=vecs[0:4, :], in_=ln_w.rearrange("(a c) -> a c", a=4))
-        nc.scalar.dma_start(out=vecs[4:8, :], in_=ln_b.rearrange("(a c) -> a c", a=4))
-        nc.scalar.dma_start(out=rows[0:8, :], in_=b_hidden.rearrange("(c n) -> c n", c=8))
         wraw = [big.tile([P, 4096], BF16, tag="big", name="wraw%d" % c) for c in range(8)]
-
-        def load_w(c):
-            nc.sync.dma_start(out=wraw[c][:].rearrange("p (s w) -> p s w", s=2), in_=wv[c])
-
-        load_w(0)
-        for lo, hi in ((4, 6), (6, 8)):
-            nc.sync.dma_start(out=xr[:, lo:hi, :], in_=xv[:, lo:hi, :])
-        warm = const.tile([P, 8], F32, name="warm")
-        nc.scalar.activation(out=warm[:], in_=mhalf[:], func=ACT.Silu)
-        nc.scalar.dma_start(out=rows[8:9, 0:256], in_=gamma.rearrange("(o a) f -> o (a f)", o=1))
-        nc.scalar.dma_start(out=rows[8:9, 256:512], in_=beta.rearrange("(o a) f -> o (a f)", o=1))
-        nc.scalar.dma_start(out=rows[9:10, 0:128], in_=b_qk.rearrange("(o f) -> o f", o=1))
-
-        load_w(1)
         wq = const.tile([P, 1024], BF16, name="wq")
-        nc.sync.dma_start(out=wq[:], in_=W_qk)
-        for c in range(2, 8):
-            load_w(c)
+        warm = const.tile([P, 8], F32, name="warm")
 
-        pv = accp.tile([P, 512], F32, tag="acc", name="pv")
-        nc.tensor.transpose(pv[:, 0:128], vecs[:].bitcast(F32), ident[:])
-        wb = const.tile([P, 16], F32, name="wb")
         bias_bc = const.tile([P, 4096], BF16, name="bias_bc")
-        qkc = const.tile([P, 1024], F32, name="qkc")
-        for i in range(5):
+        qkc = const.tile([P, 1024], QKDT, name="qkc")
+
+        def load(what, a, b):
+            if what == "x":
+                nc.sync.dma_start(out=xr[:, a:b, :], in_=xv[:, a:b, :])
+            elif what == "w":
+                nc.sync.dma_start(out=wraw[a][:].rearrange("p (s w) -> p s w", s=2), in_=wv[a])
+            elif what == "wh":
+                nc.sync.dma_start(out=wraw[a][:, 2048 * b : 2048 * b + 2048], in_=wv[a][:, b, :])
+            elif what == "wq":
+                nc.sync.dma_start(out=wq[:], in_=W_qk)
+            elif what == "vec":
+                nc.sync.dma_start(out=vecs[0:4, :], in_=ln_w.rearrange("(a c) -> a c", a=4))
+                nc.sync.dma_start(out=vecs[4:8, :], in_=ln_b.rearrange("(a c) -> a c", a=4))
+            elif what == "bh":
+                nc.sync.dma_start(out=rows[0:8, :], in_=b_hidden.rearrange("(c n) -> c n", c=8))
+            elif what == "bias":
+                nc.sync.dma_start(out=bias_bc[:], in_=b_hidden.partition_broadcast(P))
+            elif what == "qkc":
+                nc.sync.dma_start(out=qkc[:, 0:256], in_=gamma.rearrange("a f -> (a f)").partition_broadcast(P))
+                nc.sync.dma_start(out=qkc[:, 256:512], in_=beta.rearrange("a f -> (a f)").partition_broadcast(P))
+                nc.sync.dma_start(out=qkc[:, 512:640], in_=b_qk.partition_broadcast(P))
+            elif what == "qkv":
+                nc.sync.dma_start(out=rowq[0:1, 0:256], in_=gamma.rearrange("(o a) f -> o (a f)", o=1))
+                nc.sync.dma_start(out=rowq[0:1, 256:512], in_=beta.rearrange("(o a) f -> o (a f)", o=1))
+                nc.sync.dma_start(out=rowq[1:2, 0:128], in_=b_qk.rearrange("(o f) -> o f", o=1))
+
+        wb = const.tile([P, 16], F32, name="wb")
+        pvs = [None]
+
+        def pv_t():
+            pvs[0] = accp.tile([P, 512], F32, tag="acc", name="pv")
+            nc.tensor.transpose(pvs[0][:, 0:128], vecs[:].bitcast(F32), ident[:])
+
+        def bias(i, e):
             pb = tp.tile([P, 1024], BF16, tag="tp", name="pb%d" % i)
             for s in range(2):
-                r = 2 * i + s
+                r = (2 * i + s) % 8
                 nc.tensor.matmul(
                     out=pb[:, 512 * s : 512 * s + 512],
                     lhsT=identb[:, r : r + 1].to_broadcast([P, P]),
-                    rhs=rows[:],
+                    rhs=rows[:] if i < 4 else rowq[:],
                     start=True,
                     stop=True,
                 )
             dst = bias_bc[:, 1024 * i : 1024 * i + 1024] if i < 4 else qkc[:]
-            nc.scalar.copy(out=dst, in_=pb[:])
+            if e == "S":
+                nc.scalar.copy(out=dst, in_=pb[:])
+            else:
+                nc.vector.tensor_copy(out=dst, in_=pb[:])
 
         stats = const.tile([P, 8, 12], F32, name="stats")
         mv = const.tile([P, 8, 2], F32, name="mv")
         ve = const.tile([P, 8], F32, name="ve")
-        negmu = const.tile([P, 8], F32, name="negmu")
         rstd = const.tile([P, 8], F32, name="rstd")
+        nmr = const.tile([P, 8], F32, name="nmr")
+        negmu = const.tile([P, 8], F32, name="negmu")
         xh = [None] * 8
         planes = [None] * 2
         gn = [const.tile([P, 4096], BF16, name="gn%d" % h, align_bytes=64) for h in range(2)]
@@ -112,54 +141,79 @@ def tile_gau_pb_kernel(
                 nc.vector.bn_stats(out=stats[:, m, 6 * s : 6 * s + 6], in_=xr[:, m, 512 * s : 512 * s + 512])
             nc.vector.bn_aggr(out=mv[:, m, :], in_=stats[:, m, :])
 
-        def row_scalars(a, b):
+        def row_scalars(a, b, withs):
+            nc.gpsimd.tensor_scalar(out=ve[:, a:b], in0=mv[:, a:b, 1], scalar1=1.0, scalar2=EPS, op0=ALU.mult, op1=ALU.add)
+            nc.gpsimd.tensor_tensor(out=rstd[:, a:b], in0=ve[:, a:b], in1=mhalf[:, a:b], op=ALU.pow)
+            nc.gpsimd.tensor_scalar(out=negmu[:, a:b], in0=mv[:, a:b, 0], scalar1=-1.0, scalar2=0.0, op0=ALU.mult, op1=ALU.add)
+            if withs:
+                nc.gpsimd.tensor_tensor(out=nmr[:, a:b], in0=negmu[:, a:b], in1=rstd[:, a:b], op=ALU.mult)
+
+        def row_scalars_v(a, b):
             nc.vector.tensor_scalar(out=ve[:, a:b], in0=mv[:, a:b, 1], scalar1=EPS, scalar2=None, op0=ALU.add)
             nc.vector.tensor_scalar(out=negmu[:, a:b], in0=mv[:, a:b, 0], scalar1=-1.0, scalar2=None, op0=ALU.mult)
-
-        def row_rstd(a, b):
             nc.gpsimd.tensor_tensor(out=rstd[:, a:b], in0=ve[:, a:b], in1=mhalf[:, a:b], op=ALU.pow)
 
-        def normalise(m, engine):
+        def normalise(m, e):
             t = xhp.tile([P, 1024], F32, tag="xh", name="xh%d" % m)
             xh[m] = t
-            engine.tensor_scalar(
-                out=t[:].rearrange("p (a e q) -> p a e q", a=4, e=2),
-                in0=xr[:, m, :].rearrange("p (a q e) -> p a e q", a=4, e=2),
-                scalar1=negmu[:, m : m + 1],
-                scalar2=rstd[:, m : m + 1],
-                op0=ALU.add,
-                op1=ALU.mult,
-            )
+            dst = t[:].rearrange("p (a e q) -> p a e q", a=4, e=2)
+            src = xr[:, m, :].rearrange("p (a q e) -> p a e q", a=4, e=2)
+            if e == "S":
+                nc.scalar.activation(out=dst, in_=src, func=ACT.Identity, bias=nmr[:, m : m + 1], scale=rstd[:, m : m + 1])
+            else:
+                eng[e].tensor_scalar(
+                    out=dst, in0=src, scalar1=negmu[:, m : m + 1], scalar2=rstd[:, m : m + 1], op0=ALU.add, op1=ALU.mult
+                )
 
-        def x_bunch(h, g, engines):
-            if g == 0:
-                planes[h] = plp.tile([P, 8, 512], BF16, tag="pl", name="planes%d" % h)
-            banks = []
-            for t in range(4):
-                j = 4 * g + t
-                bank = tp.tile([P, 512], F32, tag="tp", name="xb%d_%d" % (h, j))
+        xbanks = {}
+
+        def x_t(h, lo, hi, pool):
+            for j in range(lo, hi):
+                if pool == "a":
+                    bank = accp.tile([P, 512], F32, tag="acc", name="xb%d_%d" % (h, j))
+                else:
+                    bank = tp.tile([P, 512], F32, tag="tp", name="xb%d_%d" % (h, j))
                 for mm in range(4):
                     nc.tensor.transpose(
                         bank[:, 128 * mm : 128 * mm + 128], xh[4 * h + mm][:, 128 * j : 128 * j + 128], ident[:]
                     )
-                banks.append(bank)
-            for t in range(4):
-                j = 4 * g + t
+                xbanks[(h, j)] = bank
+
+        def x_tt(h, mm, g, pool):
+            for j in range(4 * g, 4 * g + 4):
+                if mm == 0:
+                    if pool == "a":
+                        xbanks[(h, j)] = accp.tile([P, 512], F32, tag="acc", name="xb%d_%d" % (h, j))
+                    else:
+                        xbanks[(h, j)] = tp.tile([P, 512], F32, tag="tp", name="xb%d_%d" % (h, j))
+                nc.tensor.transpose(
+                    xbanks[(h, j)][:, 128 * mm : 128 * mm + 128], xh[4 * h + mm][:, 128 * j : 128 * j + 128], ident[:]
+                )
+
+        def x_c(h, lo, engines):
+            if planes[h] is None:
+                planes[h] = plp.tile([P, 8, 512], BF16, tag="pl", name="planes%d" % h)
+            for t in range(len(engines)):
+                j = lo + t
                 if engines[t] == "S":
                     nc.scalar.activation(
-                        out=planes[h][:, j, :], in_=banks[t][:], func=ACT.Identity,
+                        out=planes[h][:, j, :], in_=xbanks[(h, j)][:], func=ACT.Identity,
                         bias=wb[:, 8 + j : 9 + j], scale=wb[:, j : j + 1],
                     )
                 else:
                     nc.vector.tensor_scalar(
-                        out=planes[h][:, j, :], in0=banks[t][:], scalar1=wb[:, j : j + 1], scalar2=wb[:, 8 + j : 9 + j],
+                        out=planes[h][:, j, :], in0=xbanks[(h, j)][:], scalar1=wb[:, j : j + 1], scalar2=wb[:, 8 + j : 9 + j],
                         op0=ALU.mult, op1=ALU.add,
                     )
 
-        def regroup(h, g):
+        def x_bunch(h, g, engines):
+            x_t(h, 4 * g, 4 * g + 4, "t")
+            x_c(h, 4 * g, engines)
+
+        def regroup(h, g, e):
             dst = gn[h][:].rearrange("p (g c i t) -> p g c t i", g=2, i=4, t=4)[:, g]
             src = planes[h][:, 4 * g : 4 * g + 4, :].rearrange("p t (c i) -> p c t i", i=4)
-            if h == 0:
+            if e == "V":
                 nc.vector.tensor_copy(out=dst, in_=src)
             else:
                 nc.gpsimd.tensor_scalar(out=dst, in0=src, scalar1=1.0, scalar2=0.0, op0=ALU.mult, op1=ALU.add)
@@ -167,19 +221,23 @@ def tile_gau_pb_kernel(
         def quant_n(h):
             nc.vector.quantize_mx(out=cn[h][:].bitcast(FP8X4), scales=sn[h][:], in_=gn[h][:])
 
+        def quant_nh(h, g):
+            nc.vector.quantize_mx(
+                out=cn[h][:, 512 * g : 512 * g + 512].bitcast(FP8X4), scales=sn[h][:, 512 * g : 512 * g + 512],
+                in_=gn[h][:, 2048 * g : 2048 * g + 2048],
+            )
+
         cw = [const.tile([P, 1024], U32, name="cw%d" % c, align_bytes=64) for c in range(8)]
         sw = [const.tile([P, 1024], U8, name="sw%d" % c, align_bytes=64) for c in range(8)]
         cq = const.tile([P, 256], U32, name="cq", align_bytes=64)
         sq = const.tile([P, 256], U8, name="sq", align_bytes=64)
         gws = [None] * 8
 
-        def w_bunch(c, engines):
+        wbanks = {}
+
+        def w_t(c, bs):
             w32 = wraw[c][:].bitcast(F32)
-            gw = gwp.tile([P, 4096], BF16, tag="gw", name="gw%d" % c, align_bytes=64)
-            gws[c] = gw
-            gw32 = gw[:].bitcast(F32).rearrange("p (b q i u) -> p b q i u", b=4, i=2, u=2)
-            banks = []
-            for b in range(4):
+            for b in bs:
                 g, a = b // 2, b % 2
                 bank = tp.tile([P, 512], F32, tag="tp", name="wb%d_%d" % (c, b))
                 for i in range(2):
@@ -187,35 +245,49 @@ def tile_gau_pb_kernel(
                         col = (2 * a + i) * 512 + 256 * g + 128 * u
                         s = 2 * i + u
                         nc.tensor.transpose(bank[:, 128 * s : 128 * s + 128], w32[:, col : col + 128], ident[:])
-                banks.append(bank)
-            for b in range(4):
-                src = banks[b][:].rearrange("p (i u q) -> p q i u", i=2, u=2)
-                if engines[b] == "S":
+                wbanks[(c, b)] = bank
+
+        def w_c(c, bs, engines):
+            if gws[c] is None:
+                gws[c] = gwp.tile([P, 4096], BF16, tag="gw", name="gw%d" % c, align_bytes=64)
+            gw32 = gws[c][:].bitcast(F32).rearrange("p (b q i u) -> p b q i u", b=4, i=2, u=2)
+            for b, en in zip(bs, engines):
+                src = wbanks[(c, b)][:].rearrange("p (i u q) -> p q i u", i=2, u=2)
+                if en == "S":
                     nc.scalar.copy(out=gw32[:, b], in_=src)
                 else:
                     nc.vector.tensor_copy(out=gw32[:, b], in_=src)
+
+        def w_bunch(c, engines, lo=0, hi=4):
+            w_t(c, list(range(lo, hi)))
+            w_c(c, list(range(lo, hi)), engines)
 
         def quant_w(c):
             nc.vector.quantize_mx(out=cw[c][:].bitcast(FP8X4), scales=sw[c][:], in_=gws[c][:])
 
         gq = const.tile([P, 1024], BF16, name="gq", align_bytes=64)
 
-        def qk_bunch():
+        def qk_bunch(e):
             w32 = wq[:].bitcast(F32)
             bank = tp.tile([P, 512], F32, tag="tp", name="qb")
             for s in range(4):
                 nc.tensor.transpose(bank[:, 128 * s : 128 * s + 128], w32[:, 128 * s : 128 * s + 128], ident[:])
-            nc.scalar.copy(
-                out=gq[:].bitcast(F32).rearrange("p (g f u) -> p g f u", g=2, u=2),
-                in_=bank[:].rearrange("p (g u f) -> p g f u", g=2, u=2),
-            )
+            dst = gq[:].bitcast(F32).rearrange("p (g f u) -> p g f u", g=2, u=2)
+            src = bank[:].rearrange("p (g u f) -> p g f u", g=2, u=2)
+            if e == "S":
+                nc.scalar.copy(out=dst, in_=src)
+            else:
+                nc.vector.tensor_copy(out=dst, in_=src)
 
         def quant_qk():
             nc.vector.quantize_mx(out=cq[:].bitcast(FP8X4), scales=sq[:], in_=gq[:])
 
-        def unit(c, h):
+        def unit(c, h, widths):
             z = big.tile([P, 2048], F32, tag="big", name="z%d_%d" % (c, h))
             cc = c % 4
+            ends = []
+            for w in widths:
+                ends.append((ends[-1] if ends else 0) + w)
             for mm in range(4):
                 acc = accp.tile([P, 512], F32, tag="acc", name="acc%d_%d_%d" % (c, h, mm))
                 for g in range(2):
@@ -232,8 +304,8 @@ def tile_gau_pb_kernel(
                 nc.vector.tensor_tensor(
                     out=z[:, 512 * mm : 512 * mm + 512], in0=acc[:], in1=bias_bc[:, 512 * c : 512 * c + 512], op=ALU.add
                 )
-                n = 1 if (c == 7 and h == 1 and mm >= 2) else 2 * (mm % 2)
-                if n > 0:
+                if mm + 1 in ends:
+                    n = widths[ends.index(mm + 1)]
                     first = mm + 1 - n
                     part = z[:, 512 * first : 512 * (mm + 1)]
                     nc.scalar.activation(out=part, in_=part, func=ACT.Silu)
@@ -241,6 +313,41 @@ def tile_gau_pb_kernel(
                         out=ov[c // 4][:, 4 * h + first : 4 * h + mm + 1, 512 * cc : 512 * cc + 512],
                         in_=part.rearrange("p (m f) -> p m f", m=n),
                     )
+
+        zs_ = {}
+
+        def unit_a(c, h):
+            z = big.tile([P, 2048], F32, tag="big", name="z%d_%d" % (c, h))
+            zs_[(c, h)] = z
+            for mm in range(4):
+                acc = accp.tile([P, 512], F32, tag="acc", name="acc%d_%d_%d" % (c, h, mm))
+                for g in range(2):
+                    lo = 512 * g + 128 * mm
+                    nc.tensor.matmul_mx(
+                        out=acc[:],
+                        lhsT=cn[h][:, lo : lo + 128].bitcast(FP8X4),
+                        lhsT_scale=sn[h][:, lo : lo + 128],
+                        rhs=cw[c][:, 512 * g : 512 * g + 512].bitcast(FP8X4),
+                        rhs_scale=sw[c][:, 512 * g : 512 * g + 512],
+                        start=(g == 0),
+                        stop=(g == 1),
+                    )
+                nc.vector.tensor_tensor(
+                    out=z[:, 512 * mm : 512 * mm + 512], in0=acc[:], in1=bias_bc[:, 512 * c : 512 * c + 512], op=ALU.add
+                )
+
+        def unit_s(c, h, widths):
+            z = zs_[(c, h)]
+            cc = c % 4
+            first = 0
+            for n in widths:
+                part = z[:, 512 * first : 512 * (first + n)]
+                nc.scalar.activation(out=part, in_=part, func=ACT.Silu)
+                nc.sync.dma_start(
+                    out=ov[c // 4][:, 4 * h + first : 4 * h + first + n, 512 * cc : 512 * cc + 512],
+                    in_=part.rearrange("p (m f) -> p m f", m=n),
+                )
+                first += n
 
         zq = const.tile([P, 1024], F32, name="zq")
 
@@ -286,65 +393,67 @@ def tile_gau_pb_kernel(
             for i in range(2):
                 nc.sync.dma_start(out=oq[i], in_=qk[0][:, 1024 * i : 1024 * i + 1024].rearrange("p (m f) -> p m f", m=8))
 
-        for p in range(4):
-            row_stats(2 * p)
-            row_stats(2 * p + 1)
-            row_scalars(2 * p, 2 * p + 2)
-            row_rstd(2 * p, 2 * p + 2)
-            if p == 0:
-                nc.vector.tensor_copy(out=wb[:], in_=pv[:, 0:8].bitcast(BF16))
-            if p < 2:
-                normalise(2 * p, nc.gpsimd)
-                normalise(2 * p + 1, nc.gpsimd)
-        w_bunch(0, "SSSS")
-        quant_w(0)
-        x_bunch(0, 0, "SSSV")
-        x_bunch(0, 1, "SVSS")
-        normalise(4, nc.vector)
-        w_bunch(1, "VVSS")
-        normalise(6, nc.gpsimd)
-        normalise(5, nc.gpsimd)
-        regroup(0, 0)
-        w_bunch(2, "SSVV")
-        normalise(7, nc.gpsimd)
-        qk_bunch()
-        quant_w(1)
-        x_bunch(1, 0, "SSVS")
-        w_bunch(3, "SSSS")
-        regroup(0, 1)
-        quant_n(0)
-        x_bunch(1, 1, "SSSS")
-        regroup(1, 1)
-        quant_w(2)
-        quant_w(3)
-        unit(0, 0)
-        unit(1, 0)
-        regroup(1, 0)
-        quant_qk()
-        w_bunch(4, "SSSV")
-        unit(2, 0)
-        quant_n(1)
-        quant_w(4)
-        w_bunch(5, "SSSS")
-        unit_qk(0)
-        unit_qk(1)
-        qk_scale()
-        unit(0, 1)
-        unit(1, 1)
-        unit(2, 1)
-        unit(3, 0)
-        unit(3, 1)
-        unit(4, 0)
-        quant_w(5)
-        qk_store()
-        w_bunch(6, "SVSS")
-        unit(4, 1)
-        unit(5, 0)
-        quant_w(6)
-        w_bunch(7, "SSSS")
-        unit(5, 1)
-        unit(6, 0)
-        quant_w(7)
-        unit(6, 1)
-        unit(7, 0)
-        unit(7, 1)
+        for word in ORDER.split():
+            f = word.split(".")
+            k = f[0]
+            if k == "ld":
+                load(f[1], int(f[2]) if len(f) > 2 else 0, int(f[3]) if len(f) > 3 else 0)
+            elif k == "warm":
+                nc.scalar.activation(out=warm[:], in_=mhalf[:], func=ACT.Silu)
+            elif k == "pv":
+                pv_t()
+            elif k == "wb":
+                nc.vector.tensor_copy(out=wb[:], in_=pvs[0][:, 0:8].bitcast(BF16))
+            elif k == "bias":
+                bias(int(f[1]), f[2])
+            elif k == "st":
+                row_stats(int(f[1]))
+            elif k == "sc":
+                row_scalars(int(f[1]), int(f[2]), len(f) > 3)
+            elif k == "scv":
+                row_scalars_v(int(f[1]), int(f[2]))
+            elif k == "nm":
+                normalise(int(f[1]), f[2])
+            elif k == "w":
+                if len(f) > 3:
+                    w_bunch(int(f[1]), f[2], int(f[3]), int(f[4]))
+                else:
+                    w_bunch(int(f[1]), f[2])
+            elif k == "wt":
+                w_t(int(f[1]), [int(ch) for ch in f[2]])
+            elif k == "wc":
+                w_c(int(f[1]), [int(ch) for ch in f[2]], f[3])
+            elif k == "xt":
+                x_t(int(f[1]), int(f[2]), int(f[3]), f[4] if len(f) > 4 else "t")
+            elif k == "xtt":
+                x_tt(int(f[1]), int(f[2]), int(f[3]), f[4])
+            elif k == "xc":
+                x_c(int(f[1]), int(f[2]), f[3])
+            elif k == "qnh":
+                quant_nh(int(f[1]), int(f[2]))
+            elif k == "qw":
+                quant_w(int(f[1]))
+            elif k == "xb":
+                x_bunch(int(f[1]), int(f[2]), f[3])
+            elif k == "rg":
+                regroup(int(f[1]), int(f[2]), f[3])
+            elif k == "qn":
+                quant_n(int(f[1]))
+            elif k == "qkb":
+                qk_bunch(f[1])
+            elif k == "qq":
+                quant_qk()
+            elif k == "u":
+                unit(int(f[1]), int(f[2]), [int(ch) for ch in f[3]] if len(f) > 3 else [2, 2])
+            elif k == "ua":
+                unit_a(int(f[1]), int(f[2]))
+            elif k == "us":
+                unit_s(int(f[1]), int(f[2]), [int(ch) for ch in f[3]] if len(f) > 3 else [2, 2])
+            elif k == "uq":
+                unit_qk(int(f[1]))
+            elif k == "qks":
+                qk_scale()
+            elif k == "qkst":
+                qk_store()
+            else:
+                assert False, word

@@ -19,8 +19,8 @@ ORDER = """
 ld.x.0.1 ld.bh ld.vec ld.x.1.2 ld.x.2.4 ld.w.0 ld.x.4.6 ld.x.6.8 warm ld.w.1 ld.qkv ld.wq ld.w.2 ld.w.3 ld.w.4 ld.w.5 ld.w.6 ld.w.7
 bias.0.S bias.1.S bias.2.S bias.3.S pv
 st.0 st.1 scv.0.2 wb nm.0.G nm.1.G st.2 st.3 scv.2.4 nm.2.G nm.3.G st.4 st.5 scv.4.6 st.6 st.7 scv.6.8
-w.0.SSSS qw.0 bias.4.S xb.0.0.SSSV xb.0.1.SVSS nm.4.V w.1.VVSS nm.6.G nm.5.G rg.0.0.V w.2.SSVV nm.7.G qkb.S qw.1 xb.1.0.SSVS w.3.SSSS rg.0.1.V qn.0
-xb.1.1.SSSS rg.1.1.G qw.2 qw.3 u.0.0 u.1.0 rg.1.0.G qq w.4.SSSV u.2.0 qn.1 qw.4 w.5.SSSS uq.0 uq.1 qks u.0.1 u.1.1 u.2.1 u.3.0 u.3.1 u.4.0 qw.5 qkst
+w.0.SSSS qw.0 dmx.1.2 bias.4.S dmx.2.1 warmon xb.0.0.SSSV xb.0.1.SVSS nm.4.V w.1.VVSS nm.6.G nm.5.G rg.0.0.V w.2.SSVV nm.7.G qkb.S qw.1 xb.1.0.SSVS w.3.SSSS rg.0.1.V qn.0
+xb.1.1.SSSS warmoff rg.1.1.G qw.2 qw.3 u.0.0 u.1.0 rg.1.0.G qq w.4.SSSV u.2.0 qn.1 qw.4 w.5.SSSS uq.0 uq.1 qks u.0.1 u.1.1 u.2.1 u.3.0 u.3.1 u.4.0 qw.5 qkst
 w.6.SVSS u.4.1 u.5.0 qw.6 w.7.SSSS u.5.1 u.6.0 qw.7 u.6.1 u.7.0 u.7.1.211
 """
 
@@ -124,6 +124,21 @@ def tile_gau_pb_kernel(
             else:
                 nc.vector.tensor_copy(out=dst, in_=pb[:])
 
+        scr = [None]
+        warmon = [False]
+
+        def dummy(n):
+            if scr[0] is None:
+                scr[0] = accp.tile([P, 512], F32, tag="acc", name="scratch")
+            for k in range(n):
+                nc.tensor.matmul(out=scr[0][:], lhsT=identb[:], rhs=rows[:], start=True, stop=True)
+
+        def dummy_x(m, n):
+            if scr[0] is None:
+                scr[0] = accp.tile([P, 512], F32, tag="acc", name="scratch")
+            for k in range(n):
+                nc.tensor.matmul(out=scr[0][:, 0:256], lhsT=ident[:], rhs=xh[m][:, 0:256], start=True, stop=True)
+
         stats = const.tile([P, 8, 12], F32, name="stats")
         mv = const.tile([P, 8, 2], F32, name="mv")
         ve = const.tile([P, 8], F32, name="ve")
@@ -148,10 +163,19 @@ def tile_gau_pb_kernel(
             if withs:
                 nc.gpsimd.tensor_tensor(out=nmr[:, a:b], in0=negmu[:, a:b], in1=rstd[:, a:b], op=ALU.mult)
 
-        def row_scalars_v(a, b):
+        def row_scalars_v(a, b, withs=False):
             nc.vector.tensor_scalar(out=ve[:, a:b], in0=mv[:, a:b, 1], scalar1=EPS, scalar2=None, op0=ALU.add)
             nc.vector.tensor_scalar(out=negmu[:, a:b], in0=mv[:, a:b, 0], scalar1=-1.0, scalar2=None, op0=ALU.mult)
             nc.gpsimd.tensor_tensor(out=rstd[:, a:b], in0=ve[:, a:b], in1=mhalf[:, a:b], op=ALU.pow)
+            if withs:
+                nc.gpsimd.tensor_tensor(out=nmr[:, a:b], in0=negmu[:, a:b], in1=rstd[:, a:b], op=ALU.mult)
+
+        def row_scalars_s(a, b, withs=False):
+            nc.scalar.activation(out=ve[:, a:b], in_=mv[:, a:b, 1], func=ACT.Copy, bias=EPS, scale=1.0)
+            nc.scalar.activation(out=negmu[:, a:b], in_=mv[:, a:b, 0], func=ACT.Copy, bias=0.0, scale=-1.0)
+            nc.gpsimd.tensor_tensor(out=rstd[:, a:b], in0=ve[:, a:b], in1=mhalf[:, a:b], op=ALU.pow)
+            if withs:
+                nc.gpsimd.tensor_tensor(out=nmr[:, a:b], in0=negmu[:, a:b], in1=rstd[:, a:b], op=ALU.mult)
 
         def normalise(m, e):
             t = xhp.tile([P, 1024], F32, tag="xh", name="xh%d" % m)
@@ -178,6 +202,8 @@ def tile_gau_pb_kernel(
                         bank[:, 128 * mm : 128 * mm + 128], xh[4 * h + mm][:, 128 * j : 128 * j + 128], ident[:]
                     )
                 xbanks[(h, j)] = bank
+                if warmon[0] and j % 2 == 1:
+                    dummy(1)
 
         def x_tt(h, mm, g, pool):
             for j in range(4 * g, 4 * g + 4):
@@ -215,6 +241,8 @@ def tile_gau_pb_kernel(
             src = planes[h][:, 4 * g : 4 * g + 4, :].rearrange("p t (c i) -> p c t i", i=4)
             if e == "V":
                 nc.vector.tensor_copy(out=dst, in_=src)
+            elif e == "S":
+                nc.scalar.copy(out=dst, in_=src)
             else:
                 nc.gpsimd.tensor_scalar(out=dst, in0=src, scalar1=1.0, scalar2=0.0, op0=ALU.mult, op1=ALU.add)
 
@@ -246,6 +274,8 @@ def tile_gau_pb_kernel(
                         s = 2 * i + u
                         nc.tensor.transpose(bank[:, 128 * s : 128 * s + 128], w32[:, col : col + 128], ident[:])
                 wbanks[(c, b)] = bank
+                if warmon[0] and b % 2 == 1:
+                    dummy(1)
 
         def w_c(c, bs, engines):
             if gws[c] is None:
@@ -349,6 +379,40 @@ def tile_gau_pb_kernel(
                 )
                 first += n
 
+        def unit_ra(m, cg):
+            z = big.tile([P, 2048], F32, tag="big", name="zr%d_%d" % (m, cg))
+            zs_[("r", m, cg)] = z
+            h, mm = m // 4, m % 4
+            for cc in range(4):
+                c = 4 * cg + cc
+                acc = accp.tile([P, 512], F32, tag="acc", name="accr%d_%d" % (m, c))
+                for g in range(2):
+                    lo = 512 * g + 128 * mm
+                    nc.tensor.matmul_mx(
+                        out=acc[:],
+                        lhsT=cn[h][:, lo : lo + 128].bitcast(FP8X4),
+                        lhsT_scale=sn[h][:, lo : lo + 128],
+                        rhs=cw[c][:, 512 * g : 512 * g + 512].bitcast(FP8X4),
+                        rhs_scale=sw[c][:, 512 * g : 512 * g + 512],
+                        start=(g == 0),
+                        stop=(g == 1),
+                    )
+                nc.vector.tensor_tensor(
+                    out=z[:, 512 * cc : 512 * cc + 512], in0=acc[:], in1=bias_bc[:, 512 * c : 512 * c + 512], op=ALU.add
+                )
+
+        def unit_rs(m, cg, widths, one):
+            z = zs_[("r", m, cg)]
+            first = 0
+            for n in widths:
+                part = z[:, 512 * first : 512 * (first + n)]
+                nc.scalar.activation(out=part, in_=part, func=ACT.Silu)
+                if not one:
+                    nc.sync.dma_start(out=ov[cg][:, m, 512 * first : 512 * (first + n)], in_=part)
+                first += n
+            if one:
+                nc.sync.dma_start(out=ov[cg][:, m, :], in_=z[:])
+
         zq = const.tile([P, 1024], F32, name="zq")
 
         def unit_qk(h):
@@ -389,9 +453,30 @@ def tile_gau_pb_kernel(
                     op=ALU.add,
                 )
 
-        def qk_store():
+        def qk_scale_h(h):
+            if qk[0] is None:
+                qk[0] = plp.tile([P, 2048], F32, tag="pl", name="qk")
+            z3 = zq[:, 512 * h : 512 * h + 512].rearrange("p (m f) -> p m f", m=4)
             for i in range(2):
-                nc.sync.dma_start(out=oq[i], in_=qk[0][:, 1024 * i : 1024 * i + 1024].rearrange("p (m f) -> p m f", m=8))
+                o3 = qk[0][:, 1024 * i + 512 * h : 1024 * i + 512 * h + 512].rearrange("p (m f) -> p m f", m=4)
+                nc.gpsimd.tensor_tensor(
+                    out=o3, in0=z3, in1=qkc[:, 128 * i : 128 * i + 128].unsqueeze(1).to_broadcast([P, 4, 128]), op=ALU.mult
+                )
+                nc.gpsimd.tensor_tensor(
+                    out=o3, in0=o3, in1=qkc[:, 256 + 128 * i : 384 + 128 * i].unsqueeze(1).to_broadcast([P, 4, 128]),
+                    op=ALU.add,
+                )
+
+        def qk_store_h(h):
+            for i in range(2):
+                nc.sync.dma_start(
+                    out=oq[i][:, 4 * h : 4 * h + 4, :],
+                    in_=qk[0][:, 1024 * i + 512 * h : 1024 * i + 512 * h + 512].rearrange("p (m f) -> p m f", m=4),
+                )
+
+        def qk_store(q=None):
+            for i in range(2):
+                (q or nc.sync).dma_start(out=oq[i], in_=qk[0][:, 1024 * i : 1024 * i + 1024].rearrange("p (m f) -> p m f", m=8))
 
         for word in ORDER.split():
             f = word.split(".")
@@ -406,12 +491,22 @@ def tile_gau_pb_kernel(
                 nc.vector.tensor_copy(out=wb[:], in_=pvs[0][:, 0:8].bitcast(BF16))
             elif k == "bias":
                 bias(int(f[1]), f[2])
+            elif k == "dm":
+                dummy(int(f[1]))
+            elif k == "dmx":
+                dummy_x(int(f[1]), int(f[2]))
+            elif k == "warmon":
+                warmon[0] = True
+            elif k == "warmoff":
+                warmon[0] = False
             elif k == "st":
                 row_stats(int(f[1]))
             elif k == "sc":
                 row_scalars(int(f[1]), int(f[2]), len(f) > 3)
             elif k == "scv":
-                row_scalars_v(int(f[1]), int(f[2]))
+                row_scalars_v(int(f[1]), int(f[2]), len(f) > 3)
+            elif k == "scs":
+                row_scalars_s(int(f[1]), int(f[2]), len(f) > 3)
             elif k == "nm":
                 normalise(int(f[1]), f[2])
             elif k == "w":
@@ -449,11 +544,23 @@ def tile_gau_pb_kernel(
                 unit_a(int(f[1]), int(f[2]))
             elif k == "us":
                 unit_s(int(f[1]), int(f[2]), [int(ch) for ch in f[3]] if len(f) > 3 else [2, 2])
+            elif k == "ra":
+                unit_ra(int(f[1]), int(f[2]))
+            elif k == "rs":
+                unit_rs(int(f[1]), int(f[2]), [int(ch) for ch in f[3]] if len(f) > 3 else [2, 2], len(f) > 4)
             elif k == "uq":
                 unit_qk(int(f[1]))
             elif k == "qks":
-                qk_scale()
+                if len(f) > 1:
+                    qk_scale_h(int(f[1]))
+                else:
+                    qk_scale()
             elif k == "qkst":
-                qk_store()
+                if len(f) > 1 and f[1] == "g":
+                    qk_store(nc.gpsimd)
+                elif len(f) > 1:
+                    qk_store_h(int(f[1]))
+                else:
+                    qk_store()
             else:
                 assert False, word

from contextlib import ExitStack

import concourse.mybir as mybir
from concourse.masks import make_identity

F32 = mybir.dt.float32
BF16 = mybir.dt.bfloat16
U32 = mybir.dt.uint32
U8 = mybir.dt.uint8
FP8X4 = mybir.dt.float8_e4m3fn_x4
ACT = mybir.ActivationFunctionType
ALU = mybir.AluOpType

P = 128
EPS = 1e-5
FLOPS = 2 * 1024 * 1024 * (4096 + 128)

ORDER = """
ld.x.0.1 ld.bh ld.vec ld.x.1.2 ld.x.2.4 ld.w.0 ld.x.4.6 ld.x.6.8 warm ld.w.1 ld.qkv ld.wq ld.w.2 ld.w.3 ld.w.4 ld.w.5 ld.w.6 ld.w.7
bias.0.S bias.1.S bias.2.S bias.3.S pv
st.0 st.1 scv.0.2 wb nm.0.G nm.1.G st.2 st.3 scv.2.4 nm.2.G nm.3.G st.4 st.5 scv.4.6 st.6 st.7 scv.6.8
w.0.SSSS qw.0 dmx.1.2 bias.4.S dmx.2.1 warmon xb.0.0.SSSV xb.0.1.SVSS nm.4.V w.1.VVSS nm.6.G nm.5.G rg.0.0.V w.2.SSVV nm.7.G qkb.S qw.1 xb.1.0.SSVS w.3.SSSS rg.0.1.V qn.0
xb.1.1.SSSS warmoff rg.1.1.G qw.2 qw.3 u.0.0 u.1.0 rg.1.0.G qq w.4.SSSV u.2.0 qn.1 qw.4 w.5.SSSS uq.0 uq.1 qks u.0.1 u.1.1 u.2.1 u.3.0 u.3.1 u.4.0 qw.5 qkst
w.6.SVSS u.4.1 u.5.0 qw.6 w.7.SSSS u.5.1 u.6.0 qw.7 u.6.1 u.7.0 u.7.1.211
"""

QKDT = F32 if "ld.qkv" in ORDER else BF16


def tile_gau_pb_kernel(
    tc, x, ln_w, ln_b, W_hidden, b_hidden, W_qk, b_qk, gamma, beta, out_0, out_1, out_2, out_3
):
    nc = tc.nc
    xv = x.rearrange("o (p m) k -> p (o m) k", m=8)
    wv = W_hidden.rearrange("(c s q i) k -> c q s (i k)", c=8, s=2, i=2)
    ov = [
        out_0.rearrange("o (p m) f -> p (o m) f", m=8),
        out_1.rearrange("o (p m) f -> p (o m) f", m=8),
    ]
    oq = [
        out_2.rearrange("o (p m) f -> p (o m) f", m=8),
        out_3.rearrange("o (p m) f -> p (o m) f", m=8),
    ]

    with ExitStack() as ctx:
        const = ctx.enter_context(tc.tile_pool(name="const", bufs=1))
        xhp = ctx.enter_context(tc.tile_pool(name="xhp", bufs=6))
        plp = ctx.enter_context(tc.tile_pool(name="plp", bufs=2))
        big = ctx.enter_context(tc.tile_pool(name="big", bufs=8))
        gwp = ctx.enter_context(tc.tile_pool(name="gwp", bufs=2))
        tp = ctx.enter_context(tc.psum_pool(name="tp", bufs=4))
        accp = ctx.enter_context(tc.psum_pool(name="accp", bufs=4))
        ctx.enter_context(tc.manual_schedule())

        eng = {"S": nc.scalar, "V": nc.vector, "G": nc.gpsimd}

        rows = const.tile([P, 512], BF16, name="rows")
        nc.vector.memset(rows[:], 0.0)
        vecs = const.tile([P, 256], BF16, name="vecs")
        nc.vector.memset(vecs[:], 0.0)
        rowq = const.tile([P, 512], BF16, name="rowq")
        if "ld.qkv" in ORDER:
            nc.vector.memset(rowq[:], 0.0)
        mhalf = const.tile([P, 8], F32, name="mhalf")
        nc.vector.memset(mhalf[:], -0.5)
        ident = const.tile([P, P], F32, name="ident")
        make_identity(nc, ident[:])
        identb = const.tile([P, P], BF16, name="identb")
        nc.vector.tensor_copy(out=identb[:], in_=ident[:])
        xr = const.tile([P, 8, 1024], BF16, name="xr")
        wraw = [big.tile([P, 4096], BF16, tag="big", name="wraw%d" % c) for c in range(8)]
        wq = const.tile([P, 1024], BF16, name="wq")
        warm = const.tile([P, 8], F32, name="warm")

        bias_bc = const.tile([P, 4096], BF16, name="bias_bc")
        qkc = const.tile([P, 1024], QKDT, name="qkc")

        def load(what, a, b):
            if what == "x":
                nc.sync.dma_start(out=xr[:, a:b, :], in_=xv[:, a:b, :])
            elif what == "w":
                nc.sync.dma_start(out=wraw[a][:].rearrange("p (s w) -> p s w", s=2), in_=wv[a])
            elif what == "wh":
                nc.sync.dma_start(out=wraw[a][:, 2048 * b : 2048 * b + 2048], in_=wv[a][:, b, :])
            elif what == "wq":
                nc.sync.dma_start(out=wq[:], in_=W_qk)
            elif what == "vec":
                nc.sync.dma_start(out=vecs[0:4, :], in_=ln_w.rearrange("(a c) -> a c", a=4))
                nc.sync.dma_start(out=vecs[4:8, :], in_=ln_b.rearrange("(a c) -> a c", a=4))
            elif what == "bh":
                nc.sync.dma_start(out=rows[0:8, :], in_=b_hidden.rearrange("(c n) -> c n", c=8))
            elif what == "bias":
                nc.sync.dma_start(out=bias_bc[:], in_=b_hidden.partition_broadcast(P))
            elif what == "qkc":
                nc.sync.dma_start(out=qkc[:, 0:256], in_=gamma.rearrange("a f -> (a f)").partition_broadcast(P))
                nc.sync.dma_start(out=qkc[:, 256:512], in_=beta.rearrange("a f -> (a f)").partition_broadcast(P))
                nc.sync.dma_start(out=qkc[:, 512:640], in_=b_qk.partition_broadcast(P))
            elif what == "qkv":
                nc.sync.dma_start(out=rowq[0:1, 0:256], in_=gamma.rearrange("(o a) f -> o (a f)", o=1))
                nc.sync.dma_start(out=rowq[0:1, 256:512], in_=beta.rearrange("(o a) f -> o (a f)", o=1))
                nc.sync.dma_start(out=rowq[1:2, 0:128], in_=b_qk.rearrange("(o f) -> o f", o=1))

        wb = const.tile([P, 16], F32, name="wb")
        pvs = [None]

        def pv_t():
            pvs[0] = accp.tile([P, 512], F32, tag="acc", name="pv")
            nc.tensor.transpose(pvs[0][:, 0:128], vecs[:].bitcast(F32), ident[:])

        def bias(i, e):
            pb = tp.tile([P, 1024], BF16, tag="tp", name="pb%d" % i)
            for s in range(2):
                r = (2 * i + s) % 8
                nc.tensor.matmul(
                    out=pb[:, 512 * s : 512 * s + 512],
                    lhsT=identb[:, r : r + 1].to_broadcast([P, P]),
                    rhs=rows[:] if i < 4 else rowq[:],
                    start=True,
                    stop=True,
                )
            dst = bias_bc[:, 1024 * i : 1024 * i + 1024] if i < 4 else qkc[:]
            if e == "S":
                nc.scalar.copy(out=dst, in_=pb[:])
            else:
                nc.vector.tensor_copy(out=dst, in_=pb[:])

        scr = [None]
        warmon = [False]

        def dummy(n):
            if scr[0] is None:
                scr[0] = accp.tile([P, 512], F32, tag="acc", name="scratch")
            for k in range(n):
                nc.tensor.matmul(out=scr[0][:], lhsT=identb[:], rhs=rows[:], start=True, stop=True)

        def dummy_x(m, n):
            if scr[0] is None:
                scr[0] = accp.tile([P, 512], F32, tag="acc", name="scratch")
            for k in range(n):
                nc.tensor.matmul(out=scr[0][:, 0:256], lhsT=ident[:], rhs=xh[m][:, 0:256], start=True, stop=True)

        stats = const.tile([P, 8, 12], F32, name="stats")
        mv = const.tile([P, 8, 2], F32, name="mv")
        ve = const.tile([P, 8], F32, name="ve")
        rstd = const.tile([P, 8], F32, name="rstd")
        nmr = const.tile([P, 8], F32, name="nmr")
        negmu = const.tile([P, 8], F32, name="negmu")
        xh = [None] * 8
        planes = [None] * 2
        gn = [const.tile([P, 4096], BF16, name="gn%d" % h, align_bytes=64) for h in range(2)]
        cn = [const.tile([P, 1024], U32, name="cn%d" % h, align_bytes=64) for h in range(2)]
        sn = [const.tile([P, 1024], U8, name="sn%d" % h, align_bytes=64) for h in range(2)]

        def row_stats(m):
            for s in range(2):
                nc.vector.bn_stats(out=stats[:, m, 6 * s : 6 * s + 6], in_=xr[:, m, 512 * s : 512 * s + 512])
            nc.vector.bn_aggr(out=mv[:, m, :], in_=stats[:, m, :])

        def row_scalars(a, b, withs):
            nc.gpsimd.tensor_scalar(out=ve[:, a:b], in0=mv[:, a:b, 1], scalar1=1.0, scalar2=EPS, op0=ALU.mult, op1=ALU.add)
            nc.gpsimd.tensor_tensor(out=rstd[:, a:b], in0=ve[:, a:b], in1=mhalf[:, a:b], op=ALU.pow)
            nc.gpsimd.tensor_scalar(out=negmu[:, a:b], in0=mv[:, a:b, 0], scalar1=-1.0, scalar2=0.0, op0=ALU.mult, op1=ALU.add)
            if withs:
                nc.gpsimd.tensor_tensor(out=nmr[:, a:b], in0=negmu[:, a:b], in1=rstd[:, a:b], op=ALU.mult)

        def row_scalars_v(a, b, withs=False):
            nc.vector.tensor_scalar(out=ve[:, a:b], in0=mv[:, a:b, 1], scalar1=EPS, scalar2=None, op0=ALU.add)
            nc.vector.tensor_scalar(out=negmu[:, a:b], in0=mv[:, a:b, 0], scalar1=-1.0, scalar2=None, op0=ALU.mult)
            nc.gpsimd.tensor_tensor(out=rstd[:, a:b], in0=ve[:, a:b], in1=mhalf[:, a:b], op=ALU.pow)
            if withs:
                nc.gpsimd.tensor_tensor(out=nmr[:, a:b], in0=negmu[:, a:b], in1=rstd[:, a:b], op=ALU.mult)

        def row_scalars_s(a, b, withs=False):
            nc.scalar.activation(out=ve[:, a:b], in_=mv[:, a:b, 1], func=ACT.Copy, bias=EPS, scale=1.0)
            nc.scalar.activation(out=negmu[:, a:b], in_=mv[:, a:b, 0], func=ACT.Copy, bias=0.0, scale=-1.0)
            nc.gpsimd.tensor_tensor(out=rstd[:, a:b], in0=ve[:, a:b], in1=mhalf[:, a:b], op=ALU.pow)
            if withs:
                nc.gpsimd.tensor_tensor(out=nmr[:, a:b], in0=negmu[:, a:b], in1=rstd[:, a:b], op=ALU.mult)

        def normalise(m, e):
            t = xhp.tile([P, 1024], F32, tag="xh", name="xh%d" % m)
            xh[m] = t
            dst = t[:].rearrange("p (a e q) -> p a e q", a=4, e=2)
            src = xr[:, m, :].rearrange("p (a q e) -> p a e q", a=4, e=2)
            if e == "S":
                nc.scalar.activation(out=dst, in_=src, func=ACT.Identity, bias=nmr[:, m : m + 1], scale=rstd[:, m : m + 1])
            else:
                eng[e].tensor_scalar(
                    out=dst, in0=src, scalar1=negmu[:, m : m + 1], scalar2=rstd[:, m : m + 1], op0=ALU.add, op1=ALU.mult
                )

        xbanks = {}

        def x_t(h, lo, hi, pool):
            for j in range(lo, hi):
                if pool == "a":
                    bank = accp.tile([P, 512], F32, tag="acc", name="xb%d_%d" % (h, j))
                else:
                    bank = tp.tile([P, 512], F32, tag="tp", name="xb%d_%d" % (h, j))
                for mm in range(4):
                    nc.tensor.transpose(
                        bank[:, 128 * mm : 128 * mm + 128], xh[4 * h + mm][:, 128 * j : 128 * j + 128], ident[:]
                    )
                xbanks[(h, j)] = bank
                if warmon[0] and j % 2 == 1:
                    dummy(1)

        def x_tt(h, mm, g, pool):
            for j in range(4 * g, 4 * g + 4):
                if mm == 0:
                    if pool == "a":
                        xbanks[(h, j)] = accp.tile([P, 512], F32, tag="acc", name="xb%d_%d" % (h, j))
                    else:
                        xbanks[(h, j)] = tp.tile([P, 512], F32, tag="tp", name="xb%d_%d" % (h, j))
                nc.tensor.transpose(
                    xbanks[(h, j)][:, 128 * mm : 128 * mm + 128], xh[4 * h + mm][:, 128 * j : 128 * j + 128], ident[:]
                )

        def x_c(h, lo, engines):
            if planes[h] is None:
                planes[h] = plp.tile([P, 8, 512], BF16, tag="pl", name="planes%d" % h)
            for t in range(len(engines)):
                j = lo + t
                if engines[t] == "S":
                    nc.scalar.activation(
                        out=planes[h][:, j, :], in_=xbanks[(h, j)][:], func=ACT.Identity,
                        bias=wb[:, 8 + j : 9 + j], scale=wb[:, j : j + 1],
                    )
                else:
                    nc.vector.tensor_scalar(
                        out=planes[h][:, j, :], in0=xbanks[(h, j)][:], scalar1=wb[:, j : j + 1], scalar2=wb[:, 8 + j : 9 + j],
                        op0=ALU.mult, op1=ALU.add,
                    )

        def x_bunch(h, g, engines):
            x_t(h, 4 * g, 4 * g + 4, "t")
            x_c(h, 4 * g, engines)

        def regroup(h, g, e):
            dst = gn[h][:].rearrange("p (g c i t) -> p g c t i", g=2, i=4, t=4)[:, g]
            src = planes[h][:, 4 * g : 4 * g + 4, :].rearrange("p t (c i) -> p c t i", i=4)
            if e == "V":
                nc.vector.tensor_copy(out=dst, in_=src)
            elif e == "S":
                nc.scalar.copy(out=dst, in_=src)
            else:
                nc.gpsimd.tensor_scalar(out=dst, in0=src, scalar1=1.0, scalar2=0.0, op0=ALU.mult, op1=ALU.add)

        def quant_n(h):
            nc.vector.quantize_mx(out=cn[h][:].bitcast(FP8X4), scales=sn[h][:], in_=gn[h][:])

        def quant_nh(h, g):
            nc.vector.quantize_mx(
                out=cn[h][:, 512 * g : 512 * g + 512].bitcast(FP8X4), scales=sn[h][:, 512 * g : 512 * g + 512],
                in_=gn[h][:, 2048 * g : 2048 * g + 2048],
            )

        cw = [const.tile([P, 1024], U32, name="cw%d" % c, align_bytes=64) for c in range(8)]
        sw = [const.tile([P, 1024], U8, name="sw%d" % c, align_bytes=64) for c in range(8)]
        cq = const.tile([P, 256], U32, name="cq", align_bytes=64)
        sq = const.tile([P, 256], U8, name="sq", align_bytes=64)
        gws = [None] * 8

        wbanks = {}

        def w_t(c, bs):
            w32 = wraw[c][:].bitcast(F32)
            for b in bs:
                g, a = b // 2, b % 2
                bank = tp.tile([P, 512], F32, tag="tp", name="wb%d_%d" % (c, b))
                for i in range(2):
                    for u in range(2):
                        col = (2 * a + i) * 512 + 256 * g + 128 * u
                        s = 2 * i + u
                        nc.tensor.transpose(bank[:, 128 * s : 128 * s + 128], w32[:, col : col + 128], ident[:])
                wbanks[(c, b)] = bank
                if warmon[0] and b % 2 == 1:
                    dummy(1)

        def w_c(c, bs, engines):
            if gws[c] is None:
                gws[c] = gwp.tile([P, 4096], BF16, tag="gw", name="gw%d" % c, align_bytes=64)
            gw32 = gws[c][:].bitcast(F32).rearrange("p (b q i u) -> p b q i u", b=4, i=2, u=2)
            for b, en in zip(bs, engines):
                src = wbanks[(c, b)][:].rearrange("p (i u q) -> p q i u", i=2, u=2)
                if en == "S":
                    nc.scalar.copy(out=gw32[:, b], in_=src)
                else:
                    nc.vector.tensor_copy(out=gw32[:, b], in_=src)

        def w_bunch(c, engines, lo=0, hi=4):
            w_t(c, list(range(lo, hi)))
            w_c(c, list(range(lo, hi)), engines)

        def quant_w(c):
            nc.vector.quantize_mx(out=cw[c][:].bitcast(FP8X4), scales=sw[c][:], in_=gws[c][:])

        gq = const.tile([P, 1024], BF16, name="gq", align_bytes=64)

        def qk_bunch(e):
            w32 = wq[:].bitcast(F32)
            bank = tp.tile([P, 512], F32, tag="tp", name="qb")
            for s in range(4):
                nc.tensor.transpose(bank[:, 128 * s : 128 * s + 128], w32[:, 128 * s : 128 * s + 128], ident[:])
            dst = gq[:].bitcast(F32).rearrange("p (g f u) -> p g f u", g=2, u=2)
            src = bank[:].rearrange("p (g u f) -> p g f u", g=2, u=2)
            if e == "S":
                nc.scalar.copy(out=dst, in_=src)
            else:
                nc.vector.tensor_copy(out=dst, in_=src)

        def quant_qk():
            nc.vector.quantize_mx(out=cq[:].bitcast(FP8X4), scales=sq[:], in_=gq[:])

        def unit(c, h, widths):
            z = big.tile([P, 2048], F32, tag="big", name="z%d_%d" % (c, h))
            cc = c % 4
            ends = []
            for w in widths:
                ends.append((ends[-1] if ends else 0) + w)
            for mm in range(4):
                acc = accp.tile([P, 512], F32, tag="acc", name="acc%d_%d_%d" % (c, h, mm))
                for g in range(2):
                    lo = 512 * g + 128 * mm
                    nc.tensor.matmul_mx(
                        out=acc[:],
                        lhsT=cn[h][:, lo : lo + 128].bitcast(FP8X4),
                        lhsT_scale=sn[h][:, lo : lo + 128],
                        rhs=cw[c][:, 512 * g : 512 * g + 512].bitcast(FP8X4),
                        rhs_scale=sw[c][:, 512 * g : 512 * g + 512],
                        start=(g == 0),
                        stop=(g == 1),
                    )
                nc.vector.tensor_tensor(
                    out=z[:, 512 * mm : 512 * mm + 512], in0=acc[:], in1=bias_bc[:, 512 * c : 512 * c + 512], op=ALU.add
                )
                if mm + 1 in ends:
                    n = widths[ends.index(mm + 1)]
                    first = mm + 1 - n
                    part = z[:, 512 * first : 512 * (mm + 1)]
                    nc.scalar.activation(out=part, in_=part, func=ACT.Silu)
                    nc.sync.dma_start(
                        out=ov[c // 4][:, 4 * h + first : 4 * h + mm + 1, 512 * cc : 512 * cc + 512],
                        in_=part.rearrange("p (m f) -> p m f", m=n),
                    )

        zs_ = {}

        def unit_a(c, h):
            z = big.tile([P, 2048], F32, tag="big", name="z%d_%d" % (c, h))
            zs_[(c, h)] = z
            for mm in range(4):
                acc = accp.tile([P, 512], F32, tag="acc", name="acc%d_%d_%d" % (c, h, mm))
                for g in range(2):
                    lo = 512 * g + 128 * mm
                    nc.tensor.matmul_mx(
                        out=acc[:],
                        lhsT=cn[h][:, lo : lo + 128].bitcast(FP8X4),
                        lhsT_scale=sn[h][:, lo : lo + 128],
                        rhs=cw[c][:, 512 * g : 512 * g + 512].bitcast(FP8X4),
                        rhs_scale=sw[c][:, 512 * g : 512 * g + 512],
                        start=(g == 0),
                        stop=(g == 1),
                    )
                nc.vector.tensor_tensor(
                    out=z[:, 512 * mm : 512 * mm + 512], in0=acc[:], in1=bias_bc[:, 512 * c : 512 * c + 512], op=ALU.add
                )

        def unit_s(c, h, widths):
            z = zs_[(c, h)]
            cc = c % 4
            first = 0
            for n in widths:
                part = z[:, 512 * first : 512 * (first + n)]
                nc.scalar.activation(out=part, in_=part, func=ACT.Silu)
                nc.sync.dma_start(
                    out=ov[c // 4][:, 4 * h + first : 4 * h + first + n, 512 * cc : 512 * cc + 512],
                    in_=part.rearrange("p (m f) -> p m f", m=n),
                )
                first += n

        def unit_ra(m, cg):
            z = big.tile([P, 2048], F32, tag="big", name="zr%d_%d" % (m, cg))
            zs_[("r", m, cg)] = z
            h, mm = m // 4, m % 4
            for cc in range(4):
                c = 4 * cg + cc
                acc = accp.tile([P, 512], F32, tag="acc", name="accr%d_%d" % (m, c))
                for g in range(2):
                    lo = 512 * g + 128 * mm
                    nc.tensor.matmul_mx(
                        out=acc[:],
                        lhsT=cn[h][:, lo : lo + 128].bitcast(FP8X4),
                        lhsT_scale=sn[h][:, lo : lo + 128],
                        rhs=cw[c][:, 512 * g : 512 * g + 512].bitcast(FP8X4),
                        rhs_scale=sw[c][:, 512 * g : 512 * g + 512],
                        start=(g == 0),
                        stop=(g == 1),
                    )
                nc.vector.tensor_tensor(
                    out=z[:, 512 * cc : 512 * cc + 512], in0=acc[:], in1=bias_bc[:, 512 * c : 512 * c + 512], op=ALU.add
                )

        def unit_rs(m, cg, widths, one):
            z = zs_[("r", m, cg)]
            first = 0
            for n in widths:
                part = z[:, 512 * first : 512 * (first + n)]
                nc.scalar.activation(out=part, in_=part, func=ACT.Silu)
                if not one:
                    nc.sync.dma_start(out=ov[cg][:, m, 512 * first : 512 * (first + n)], in_=part)
                first += n
            if one:
                nc.sync.dma_start(out=ov[cg][:, m, :], in_=z[:])

        zq = const.tile([P, 1024], F32, name="zq")

        def unit_qk(h):
            acc = accp.tile([P, 512], F32, tag="acc", name="accq%d" % h)
            for mm in range(4):
                for g in range(2):
                    lo = 512 * g + 128 * mm
                    nc.tensor.matmul_mx(
                        out=acc[:, 128 * mm : 128 * mm + 128],
                        lhsT=cn[h][:, lo : lo + 128].bitcast(FP8X4),
                        lhsT_scale=sn[h][:, lo : lo + 128],
                        rhs=cq[:, 128 * g : 128 * g + 128].bitcast(FP8X4),
                        rhs_scale=sq[:, 128 * g : 128 * g + 128],
                        start=(g == 0),
                        stop=(g == 1),
                    )
            zs = zq[:, 512 * h : 512 * h + 512]
            nc.vector.tensor_tensor(
                out=zs.rearrange("p (m f) -> p m f", m=4),
                in0=acc[:].rearrange("p (m f) -> p m f", m=4),
                in1=qkc[:, 512:640].unsqueeze(1).to_broadcast([P, 4, 128]),
                op=ALU.add,
            )
            nc.scalar.activation(out=zs, in_=zs, func=ACT.Silu)

        qk = [None]

        def qk_scale():
            qk[0] = plp.tile([P, 2048], F32, tag="pl", name="qk")
            z3 = zq[:].rearrange("p (m f) -> p m f", m=8)
            for i in range(2):
                o3 = qk[0][:, 1024 * i : 1024 * i + 1024].rearrange("p (m f) -> p m f", m=8)
                nc.gpsimd.tensor_tensor(
                    out=o3, in0=z3, in1=qkc[:, 128 * i : 128 * i + 128].unsqueeze(1).to_broadcast([P, 8, 128]), op=ALU.mult
                )
                nc.gpsimd.tensor_tensor(
                    out=o3, in0=o3, in1=qkc[:, 256 + 128 * i : 384 + 128 * i].unsqueeze(1).to_broadcast([P, 8, 128]),
                    op=ALU.add,
                )

        def qk_scale_h(h):
            if qk[0] is None:
                qk[0] = plp.tile([P, 2048], F32, tag="pl", name="qk")
            z3 = zq[:, 512 * h : 512 * h + 512].rearrange("p (m f) -> p m f", m=4)
            for i in range(2):
                o3 = qk[0][:, 1024 * i + 512 * h : 1024 * i + 512 * h + 512].rearrange("p (m f) -> p m f", m=4)
                nc.gpsimd.tensor_tensor(
                    out=o3, in0=z3, in1=qkc[:, 128 * i : 128 * i + 128].unsqueeze(1).to_broadcast([P, 4, 128]), op=ALU.mult
                )
                nc.gpsimd.tensor_tensor(
                    out=o3, in0=o3, in1=qkc[:, 256 + 128 * i : 384 + 128 * i].unsqueeze(1).to_broadcast([P, 4, 128]),
                    op=ALU.add,
                )

        def qk_store_h(h):
            for i in range(2):
                nc.sync.dma_start(
                    out=oq[i][:, 4 * h : 4 * h + 4, :],
                    in_=qk[0][:, 1024 * i + 512 * h : 1024 * i + 512 * h + 512].rearrange("p (m f) -> p m f", m=4),
                )

        def qk_store(q=None):
            for i in range(2):
                (q or nc.sync).dma_start(out=oq[i], in_=qk[0][:, 1024 * i : 1024 * i + 1024].rearrange("p (m f) -> p m f", m=8))

        for word in ORDER.split():
            f = word.split(".")
            k = f[0]
            if k == "ld":
                load(f[1], int(f[2]) if len(f) > 2 else 0, int(f[3]) if len(f) > 3 else 0)
            elif k == "warm":
                nc.scalar.activation(out=warm[:], in_=mhalf[:], func=ACT.Silu)
            elif k == "pv":
                pv_t()
            elif k == "wb":
                nc.vector.tensor_copy(out=wb[:], in_=pvs[0][:, 0:8].bitcast(BF16))
            elif k == "bias":
                bias(int(f[1]), f[2])
            elif k == "dm":
                dummy(int(f[1]))
            elif k == "dmx":
                dummy_x(int(f[1]), int(f[2]))
            elif k == "warmon":
                warmon[0] = True
            elif k == "warmoff":
                warmon[0] = False
            elif k == "st":
                row_stats(int(f[1]))
            elif k == "sc":
                row_scalars(int(f[1]), int(f[2]), len(f) > 3)
            elif k == "scv":
                row_scalars_v(int(f[1]), int(f[2]), len(f) > 3)
            elif k == "scs":
                row_scalars_s(int(f[1]), int(f[2]), len(f) > 3)
            elif k == "nm":
                normalise(int(f[1]), f[2])
            elif k == "w":
                if len(f) > 3:
                    w_bunch(int(f[1]), f[2], int(f[3]), int(f[4]))
                else:
                    w_bunch(int(f[1]), f[2])
            elif k == "wt":
                w_t(int(f[1]), [int(ch) for ch in f[2]])
            elif k == "wc":
                w_c(int(f[1]), [int(ch) for ch in f[2]], f[3])
            elif k == "xt":
                x_t(int(f[1]), int(f[2]), int(f[3]), f[4] if len(f) > 4 else "t")
            elif k == "xtt":
                x_tt(int(f[1]), int(f[2]), int(f[3]), f[4])
            elif k == "xc":
                x_c(int(f[1]), int(f[2]), f[3])
            elif k == "qnh":
                quant_nh(int(f[1]), int(f[2]))
            elif k == "qw":
                quant_w(int(f[1]))
            elif k == "xb":
                x_bunch(int(f[1]), int(f[2]), f[3])
            elif k == "rg":
                regroup(int(f[1]), int(f[2]), f[3])
            elif k == "qn":
                quant_n(int(f[1]))
            elif k == "qkb":
                qk_bunch(f[1])
            elif k == "qq":
                quant_qk()
            elif k == "u":
                unit(int(f[1]), int(f[2]), [int(ch) for ch in f[3]] if len(f) > 3 else [2, 2])
            elif k == "ua":
                unit_a(int(f[1]), int(f[2]))
            elif k == "us":
                unit_s(int(f[1]), int(f[2]), [int(ch) for ch in f[3]] if len(f) > 3 else [2, 2])
            elif k == "ra":
                unit_ra(int(f[1]), int(f[2]))
            elif k == "rs":
                unit_rs(int(f[1]), int(f[2]), [int(ch) for ch in f[3]] if len(f) > 3 else [2, 2], len(f) > 4)
            elif k == "uq":
                unit_qk(int(f[1]))
            elif k == "qks":
                if len(f) > 1:
                    qk_scale_h(int(f[1]))
                else:
                    qk_scale()
            elif k == "qkst":
                if len(f) > 1 and f[1] == "g":
                    qk_store(nc.gpsimd)
                elif len(f) > 1:
                    qk_store_h(int(f[1]))
                else:
                    qk_store()
            else:
                assert False, word
